import numpy as np
import ml_dtypes


def mxq(x, axis, fmt="e4m3"):
    dtype, down = {"e4m3": (ml_dtypes.float8_e4m3fn, 7), "e5m2": (ml_dtypes.float8_e5m2, 14)}[fmt]
    v = np.moveaxis(np.asarray(x, np.float32).astype(ml_dtypes.bfloat16).astype(np.float64), axis, -1)
    blocks = v.reshape(v.shape[:-1] + (-1, 32))
    amax = np.abs(blocks).max(-1, keepdims=True)
    byte = np.maximum(np.where(amax > 0, np.frexp(amax)[1] - 1 + 127, 0) - down, 1)
    scale = np.exp2(byte - 127.0)
    codes = (blocks / scale).astype(np.float32).astype(dtype).astype(np.float64)
    return np.moveaxis((codes * scale).reshape(v.shape), -1, axis)


WIDE = False


def mx_kscale(k):
    if not WIDE:
        return np.ones(k)
    levels = np.array([10, -10, 5, -5, 0])
    a = np.random.permutation(np.resize(levels, k // 512 * 4)).reshape(k // 512, 4)
    idx = np.arange(k)
    return np.exp2(a[idx // 512, idx % 128 // 32])


BF16 = ml_dtypes.bfloat16


def bf(x):
    return np.asarray(x, np.float32).astype(BF16)


def f64(x):
    return np.asarray(x).astype(np.float64)


B, N, H = 4096, 512, 512
BETA = 0.99
LOG2PI = np.log(2.0 * np.pi)


def lyap(u):
    return np.sum(u * u, axis=-1, keepdims=True) + 1e-3


def setup_inputs():
    s = mx_kscale(H)
    g = np.exp(0.4 * np.random.standard_normal(B))[:, None]
    col = np.concatenate([np.full(N, 3.0), np.full(N, 0.8)])
    off = np.concatenate([np.zeros(N), np.full(N, -1.5)])
    return {"h": bf(np.tanh(np.random.standard_normal((B, H))) * s),
            "W2": bf(np.random.standard_normal((H, 2 * N)) * col / np.sqrt(H) / s[:, None]),
            "b2": bf(np.random.standard_normal(2 * N) * 0.4 + off),
            "x": bf(np.random.standard_normal((B, N)) * 1.5 * g),
            "y": bf(np.random.standard_normal((B, N))[:, None, :] * 0.7),
            "eps": bf(np.random.standard_normal((B, N))[:, None, :]),
            "Wv": bf(np.random.standard_normal((N, N)) * 0.1 / N)}


def reference(h, W2, b2, x, y, eps, Wv):
    f = (mxq(f64(h), 1, "e4m3") @ mxq(f64(W2), 0, "e4m3")) + f64(b2)
    mu, logvar = f[:, :N], f[:, N:]
    mu = mu[:, None, :]
    var = np.exp(logvar)[:, None, :]
    wvq = mxq(f64(Wv), 0, "e4m3")
    Vx = lyap(mxq(f64(x), 1, "e4m3") @ wvq)[:, None, :]
    Vmu = lyap(mxq(mu, 2, "e4m3") @ wvq)
    bVx = BETA * Vx
    mu_stable = mu * ((bVx - np.maximum(bVx - Vmu, 0.0)) / Vmu)
    fx = mu_stable + np.sqrt(var) * f64(eps)
    q = (f64(y) - mu_stable) ** 2 / var
    logp = -0.5 * (N * LOG2PI + np.sum(np.log(var) + q, axis=-1))
    return fx, logp

@@ -1,0 +1,297 @@
+from contextlib import ExitStack
+import math
+
+import concourse.bass as bass
+import concourse.mybir as mybir
+import concourse.tile as tile
+from concourse.masks import make_identity
+
+F32 = mybir.dt.float32
+BF16 = mybir.dt.bfloat16
+U32 = mybir.dt.uint32
+U8 = mybir.dt.uint8
+FP8X4 = mybir.dt.float8_e4m3fn_x4
+ALU = mybir.AluOpType
+ACT = mybir.ActivationFunctionType
+
+P = 128
+B, N, H = 4096, 512, 512
+NT = B // P
+BETA = 0.99
+FLOOR = 1e-3
+FLOPS = 2 * B * H * (2 * N) + 2 * 2 * B * N * N
+PIN = False
+LAG = 7
+
+
+def tile_mdn_module_pa_t_kernel(tc, h, W2, b2, x, y, eps, Wv, out_0, out_1):
+    nc = tc.nc
+    hv = h.rearrange("(p j) k -> p (j k)", j=NT)
+    xv = x.rearrange("(p j) k -> p (j k)", j=NT)
+    yv = y.rearrange("(p j) o k -> p (j o k)", j=NT)
+    ev = eps.rearrange("(p j) o k -> p (j o k)", j=NT)
+    fv = out_0.rearrange("(p j) o k -> p (j o k)", j=NT)
+    lv = out_1.rearrange("(p j) o -> p (j o)", j=NT)
+
+    with ExitStack() as ctx:
+        if PIN:
+            ctx.enter_context(tc.manual_schedule())
+        const = ctx.enter_context(tc.tile_pool(name="const", bufs=1))
+        stage = ctx.enter_context(tc.tile_pool(name="stage", bufs=1))
+        loads = ctx.enter_context(tc.tile_pool(name="loads", bufs=3))
+        work = ctx.enter_context(tc.tile_pool(name="work", bufs=3))
+        psum = ctx.enter_context(tc.psum_pool(name="psum", bufs=1))
+
+        w2raw = stage.tile([P, 4 * 1024], BF16, name="w2raw")
+        w2v = W2.rearrange("(u p e) c -> p u (e c)", u=2, p=P, e=2)
+        for u in range(2):
+            nc.sync.dma_start(out=w2raw[:, 2048 * u : 2048 * (u + 1)], in_=w2v[:, u, :])
+
+        hq, xq, yq, eq = {}, {}, {}, {}
+
+        def load_hx(q):
+            hq[q] = loads.tile([P, 2048], BF16, name="hq%d" % q, tag="hq")
+            nc.sync.dma_start(out=hq[q][:], in_=hv[:, 2048 * q : 2048 * (q + 1)])
+            xq[q] = loads.tile([P, 2048], BF16, name="xq%d" % q, tag="xq")
+            nc.sync.dma_start(out=xq[q][:], in_=xv[:, 2048 * q : 2048 * (q + 1)])
+
+        def load_ye(q):
+            eq[q] = loads.tile([P, 2048], BF16, name="eq%d" % q, tag="eq")
+            nc.sync.dma_start(out=eq[q][:], in_=ev[:, 2048 * q : 2048 * (q + 1)])
+            yq[q] = loads.tile([P, 2048], BF16, name="yq%d" % q, tag="yq")
+            nc.sync.dma_start(out=yq[q][:], in_=yv[:, 2048 * q : 2048 * (q + 1)])
+
+        load_hx(0)
+        wvaraw = stage.tile([P, 4 * 512], BF16, name="wvaraw")
+        nc.sync.dma_start(
+            out=wvaraw[:].rearrange("p (u f) -> p u f", u=2),
+            in_=Wv.rearrange("(u p e) c -> p u (e c)", u=2, p=P, e=2),
+        )
+        bias = const.tile([P, 2 * N], BF16, name="bias")
+        nc.sync.dma_start(out=bias[:], in_=b2.partition_broadcast(P))
+        wvbraw = stage.tile([P, 4 * 512], BF16, name="wvbraw")
+        nc.sync.dma_start(
+            out=wvbraw[:].rearrange("p (t c) -> p t c", t=4),
+            in_=Wv.rearrange("(t p) c -> p t c", p=P),
+        )
+        load_hx(1)
+
+        ident = const.tile([P, P], F32, name="ident")
+        make_identity(nc, ident[:])
+        warm = const.tile([P, 1], F32, name="warm")
+        nc.vector.memset(warm[:], 0.0)
+        nc.scalar.activation(out=warm[:], in_=warm[:], func=ACT.Exp)
+
+        w2c = const.tile([P, 1024], U32, name="w2c", align_bytes=64)
+        w2s = const.tile([P, 1024], U8, name="w2s", align_bytes=64)
+        wvac = const.tile([P, 512], U32, name="wvac", align_bytes=64)
+        wvas = const.tile([P, 512], U8, name="wvas", align_bytes=64)
+        wvbc = const.tile([P, 512], U32, name="wvbc", align_bytes=64)
+        wvbs = const.tile([P, 512], U8, name="wvbs", align_bytes=64)
+        w2g = stage.tile([P, 4096], BF16, name="w2g", align_bytes=64)
+        wvag = stage.tile([P, 2048], BF16, name="wvag", align_bytes=64)
+        wvbg = stage.tile([P, 2048], BF16, name="wvbg", align_bytes=64)
+
+        def regroup(copy, dst, src):
+            copy(
+                out=dst.rearrange("p (c i t) -> p c t i", i=4, t=4),
+                in_=src.rearrange("p t (c i) -> p c t i", i=4),
+            )
+
+        w2r3 = w2raw[:].rearrange("p (t c) -> p t c", t=4)
+        regroup(nc.vector.tensor_copy, w2g[:, 0:2048], w2r3[:, :, 0:512])
+        regroup(nc.scalar.copy, w2g[:, 2048:4096], w2r3[:, :, 512:1024])
+        regroup(nc.vector.tensor_copy, wvag[:], wvaraw[:].rearrange("p (t c) -> p t c", t=4))
+        nc.vector.quantize_mx(out=w2c[:, 0:512].bitcast(FP8X4), scales=w2s[:, 0:512], in_=w2g[:, 0:2048])
+        nc.vector.quantize_mx(out=wvac[:].bitcast(FP8X4), scales=wvas[:], in_=wvag[:])
+        nc.vector.quantize_mx(out=w2c[:, 512:1024].bitcast(FP8X4), scales=w2s[:, 512:1024], in_=w2g[:, 2048:4096])
+
+        vx = const.tile([P, NT], F32, name="vx")
+        vm = const.tile([P, NT], F32, name="vm")
+        sq = const.tile([P, NT], F32, name="sq")
+        sl = const.tile([P, NT], F32, name="sl")
+        sa = const.tile([P, NT], F32, name="sa")
+        sm = const.tile([P, NT], F32, name="sm")
+        sr = const.tile([P, NT], F32, name="sr")
+        sn = const.tile([P, NT], F32, name="sn")
+        sf = const.tile([P, NT], F32, name="sf")
+
+        tp, grp, cod, scl = {}, {}, {}, {}
+        mups, lvps, uxps, umps, mtps = {}, {}, {}, {}, {}
+        mu32, lv32, gmu, cmu, smu = {}, {}, {}, {}, {}
+        sd, isd, dd, fxp = {}, {}, {}, {}
+
+        def ok(j):
+            return 0 <= j < NT
+
+        def t_hx(j):
+            q, i = divmod(j, 4)
+            tp[j] = psum.tile([P, 512], F32, name="tp%d" % j, tag="tp", bufs=2)
+            for o, src in enumerate((hq[q], xq[q])):
+                words = src[:].bitcast(F32)
+                for u in range(2):
+                    nc.tensor.transpose(
+                        tp[j][:, (2 * o + u) * P : (2 * o + u + 1) * P],
+                        words[:, 256 * i + P * u : 256 * i + P * (u + 1)],
+                        ident[:],
+                    )
+
+        def t_mu(j):
+            mtps[j] = psum.tile([P, 512], F32, name="mt%d" % j, tag="mt", bufs=2)
+            for t in range(4):
+                nc.tensor.transpose(mtps[j][:, P * t : P * (t + 1)], mu32[j][:, P * t : P * (t + 1)], ident[:])
+
+        def mx(out, lc, ls, rc, rs):
+            nc.tensor.matmul_mx(
+                out=out, lhsT=lc.bitcast(FP8X4), lhsT_scale=ls, rhs=rc.bitcast(FP8X4), rhs_scale=rs,
+                start=True, stop=True,
+            )
+
+        def mx3(j):
+            mups[j] = psum.tile([P, 512], F32, name="mups%d" % j, tag="mups")
+            lvps[j] = psum.tile([P, 512], F32, name="lvps%d" % j, tag="lvps")
+            uxps[j] = psum.tile([P, 512], F32, name="uxps%d" % j, tag="uxps")
+            mx(mups[j][:], cod[j][:, 0:P], scl[j][:, 0:P], w2c[:, 0:512], w2s[:, 0:512])
+            mx(lvps[j][:], cod[j][:, 0:P], scl[j][:, 0:P], w2c[:, 512:1024], w2s[:, 512:1024])
+            mx(uxps[j][:], cod[j][:, P : 2 * P], scl[j][:, P : 2 * P], wvac[:], wvas[:])
+
+        def mxu(j):
+            umps[j] = psum.tile([P, 512], F32, name="umps%d" % j, tag="umps")
+            mx(umps[j][:], cmu[j][:], smu[j][:], wvbc[:], wvbs[:])
+
+        def exit_hx(j):
+            grp[j] = work.tile([P, 1024], BF16, name="grp%d" % j, tag="grp", align_bytes=64)
+            nc.scalar.copy(
+                out=grp[j][:].bitcast(F32).rearrange("p (o r u) -> p o r u", o=2, u=2),
+                in_=tp[j][:].rearrange("p (o u r) -> p o r u", o=2, u=2),
+            )
+
+        def exit_mu(j):
+            gmu[j] = work.tile([P, 512], BF16, name="gmu%d" % j, tag="gmu", align_bytes=64)
+            nc.scalar.copy(
+                out=gmu[j][:].rearrange("p (r t) -> p r t", t=4),
+                in_=mtps[j][:].rearrange("p (t r) -> p r t", t=4),
+            )
+
+        def square_sum(src, acc, j, label):
+            junk = work.tile([P, 512], BF16, name="junk%s%d" % (label, j), tag="junk", bufs=2)
+            nc.scalar.activation(out=junk[:], in_=src, func=ACT.Square, accum_out=acc[:, j : j + 1])
+
+        def exps(j):
+            sd[j] = work.tile([P, 512], F32, name="sd%d" % j, tag="sd")
+            isd[j] = work.tile([P, 512], F32, name="isd%d" % j, tag="isd")
+            nc.scalar.activation(out=sd[j][:], in_=lv32[j][:], func=ACT.Exp, scale=0.5)
+            nc.scalar.activation(out=isd[j][:], in_=lv32[j][:], func=ACT.Exp, scale=-0.5)
+
+        def quant_hx(j):
+            cod[j] = work.tile([P, 256], U32, name="cod%d" % j, tag="cod", align_bytes=64)
+            scl[j] = work.tile([P, 256], U8, name="scl%d" % j, tag="scl", align_bytes=64)
+            nc.vector.quantize_mx(out=cod[j][:].bitcast(FP8X4), scales=scl[j][:], in_=grp[j][:])
+
+        def quant_mu(j):
+            cmu[j] = work.tile([P, P], U32, name="cmu%d" % j, tag="cmu", align_bytes=64)
+            smu[j] = work.tile([P, P], U8, name="smu%d" % j, tag="smu", align_bytes=64)
+            nc.vector.quantize_mx(out=cmu[j][:].bitcast(FP8X4), scales=smu[j][:], in_=gmu[j][:])
+
+        def add_mu(j):
+            mu32[j] = work.tile([P, 512], F32, name="mu%d" % j, tag="mu32", bufs=LAG + 1)
+            nc.vector.tensor_tensor(out=mu32[j][:], in0=mups[j][:], in1=bias[:, 0:N], op=ALU.add)
+
+        def add_lv(j):
+            lv32[j] = work.tile([P, 512], F32, name="lv%d" % j, tag="lv32", bufs=LAG + 1)
+            nc.vector.scalar_tensor_tensor(
+                out=lv32[j][:], in0=lvps[j][:], scalar=1.0, in1=bias[:, N : 2 * N],
+                op0=ALU.mult, op1=ALU.add, accum_out=sl[:, j : j + 1],
+            )
+
+        def noise(c):
+            q, i = divmod(c, 4)
+            if c % 2 == 0:
+                fxp[c // 2] = work.tile([P, 1024], F32, name="fx%d" % (c // 2), tag="fx", bufs=4)
+            dst = fxp[c // 2][:, 512 * (c % 2) : 512 * (c % 2 + 1)]
+            nc.vector.tensor_tensor(out=dst, in0=sd[c][:], in1=eq[q][:, 512 * i : 512 * (i + 1)], op=ALU.mult)
+
+        def sample(c):
+            dst = fxp[c // 2][:, 512 * (c % 2) : 512 * (c % 2 + 1)]
+            nc.vector.scalar_tensor_tensor(
+                out=dst, in0=mu32[c][:], scalar=sf[:, c : c + 1], in1=dst, op0=ALU.mult, op1=ALU.add,
+            )
+
+        def resid(c):
+            q, i = divmod(c, 4)
+            dd[c] = work.tile([P, 512], F32, name="dd%d" % c, tag="dd")
+            nc.vector.scalar_tensor_tensor(
+                out=dd[c][:], in0=mu32[c][:], scalar=sf[:, c : c + 1], in1=yq[q][:, 512 * i : 512 * (i + 1)],
+                op0=ALU.mult, op1=ALU.subtract,
+            )
+
+        def whiten(c):
+            nc.vector.tensor_tensor(out=dd[c][:], in0=dd[c][:], in1=isd[c][:], op=ALU.mult)
+
+        for n in range(NT + LAG + 2):
+            c = n - LAG
+            if n % 4 == 0:
+                if n // 4 < NT // 4:
+                    load_ye(n // 4)
+                if n // 4 + 2 < NT // 4:
+                    load_hx(n // 4 + 2)
+            if ok(n):
+                t_hx(n)
+            if ok(n - 2):
+                t_mu(n - 2)
+            if ok(n - 1):
+                mx3(n - 1)
+            if ok(n - 3):
+                mxu(n - 3)
+            if ok(n):
+                exit_hx(n)
+            if ok(n - 2):
+                exit_mu(n - 2)
+            if ok(n - 1):
+                square_sum(uxps[n - 1][:], vx, n - 1, "x")
+            if ok(n - 3):
+                square_sum(umps[n - 3][:], vm, n - 3, "m")
+            if n == 0:
+                regroup(nc.scalar.copy, wvbg[:], wvbraw[:].rearrange("p (t c) -> p t c", t=4))
+            if ok(c + 1):
+                exps(c + 1)
+            if ok(c - 1):
+                square_sum(dd[c - 1][:], sq, c - 1, "q")
+            small = ok(c) and c % 4 == 0
+            cols = slice(c, c + 4)
+            if small:
+                nc.vector.tensor_scalar(
+                    out=sa[:, cols], in0=vx[:, cols], scalar1=BETA, scalar2=BETA * FLOOR, op0=ALU.mult, op1=ALU.add,
+                )
+                nc.vector.tensor_scalar_add(out=sm[:, cols], in0=vm[:, cols], scalar1=FLOOR)
+            if ok(n - 1):
+                add_mu(n - 1)
+            if small:
+                nc.vector.reciprocal(out=sr[:, cols], in_=sm[:, cols])
+                nc.vector.tensor_tensor(out=sn[:, cols], in0=sa[:, cols], in1=sm[:, cols], op=ALU.min)
+            if ok(n - 1):
+                add_lv(n - 1)
+            if small:
+                nc.vector.tensor_tensor(out=sf[:, cols], in0=sn[:, cols], in1=sr[:, cols], op=ALU.mult)
+            if ok(c):
+                noise(c)
+            if ok(n):
+                quant_hx(n)
+            if n == 1:
+                nc.vector.quantize_mx(out=wvbc[:].bitcast(FP8X4), scales=wvbs[:], in_=wvbg[:])
+            if ok(c):
+                sample(c)
+                resid(c)
+            if ok(n - 2):
+                quant_mu(n - 2)
+            if ok(c):
+                whiten(c)
+                if c % 2 == 1:
+                    nc.sync.dma_start(out=fv[:, 1024 * (c // 2) : 1024 * (c // 2 + 1)], in_=fxp[c // 2][:])
+
+        lp = const.tile([P, NT], F32, name="lp")
+        nc.vector.tensor_tensor(out=lp[:], in0=sl[:], in1=sq[:], op=ALU.add)
+        nc.vector.tensor_scalar(
+            out=lp[:], in0=lp[:], scalar1=-0.5, scalar2=-0.5 * N * math.log(2.0 * math.pi), op0=ALU.mult, op1=ALU.add,
+        )
+        nc.sync.dma_start(out=lv, in_=lp[:])

@@ -20,7 +20,7 @@ NT = B // P
 BETA = 0.99
 FLOOR = 1e-3
 FLOPS = 2 * B * H * (2 * N) + 2 * 2 * B * N * N
-PIN = False
+PIN = True
 LAG = 7
 
 
@@ -159,9 +159,9 @@ def tile_mdn_module_pa_t_kernel(tc, h, W2, b2, x, y, eps, Wv, out_0, out_1):
             umps[j] = psum.tile([P, 512], F32, name="umps%d" % j, tag="umps")
             mx(umps[j][:], cmu[j][:], smu[j][:], wvbc[:], wvbs[:])
 
-        def exit_hx(j):
+        def exit_hx(j, copy):
             grp[j] = work.tile([P, 1024], BF16, name="grp%d" % j, tag="grp", align_bytes=64)
-            nc.scalar.copy(
+            copy(
                 out=grp[j][:].bitcast(F32).rearrange("p (o r u) -> p o r u", o=2, u=2),
                 in_=tp[j][:].rearrange("p (o u r) -> p o r u", o=2, u=2),
             )
@@ -209,7 +209,7 @@ def tile_mdn_module_pa_t_kernel(tc, h, W2, b2, x, y, eps, Wv, out_0, out_1):
             if c % 2 == 0:
                 fxp[c // 2] = work.tile([P, 1024], F32, name="fx%d" % (c // 2), tag="fx", bufs=4)
             dst = fxp[c // 2][:, 512 * (c % 2) : 512 * (c % 2 + 1)]
-            nc.vector.tensor_tensor(out=dst, in0=sd[c][:], in1=eq[q][:, 512 * i : 512 * (i + 1)], op=ALU.mult)
+            nc.gpsimd.tensor_tensor(out=dst, in0=sd[c][:], in1=eq[q][:, 512 * i : 512 * (i + 1)], op=ALU.mult)
 
         def sample(c):
             dst = fxp[c // 2][:, 512 * (c % 2) : 512 * (c % 2 + 1)]
@@ -228,6 +228,9 @@ def tile_mdn_module_pa_t_kernel(tc, h, W2, b2, x, y, eps, Wv, out_0, out_1):
         def whiten(c):
             nc.vector.tensor_tensor(out=dd[c][:], in0=dd[c][:], in1=isd[c][:], op=ALU.mult)
 
+        def on_vector(j):
+            return j % 3 != 0
+
         for n in range(NT + LAG + 2):
             c = n - LAG
             if n % 4 == 0:
@@ -243,8 +246,8 @@ def tile_mdn_module_pa_t_kernel(tc, h, W2, b2, x, y, eps, Wv, out_0, out_1):
                 mx3(n - 1)
             if ok(n - 3):
                 mxu(n - 3)
-            if ok(n):
-                exit_hx(n)
+            if ok(n) and not on_vector(n):
+                exit_hx(n, nc.scalar.copy)
             if ok(n - 2):
                 exit_mu(n - 2)
             if ok(n - 1):
@@ -253,41 +256,42 @@ def tile_mdn_module_pa_t_kernel(tc, h, W2, b2, x, y, eps, Wv, out_0, out_1):
                 square_sum(umps[n - 3][:], vm, n - 3, "m")
             if n == 0:
                 regroup(nc.scalar.copy, wvbg[:], wvbraw[:].rearrange("p (t c) -> p t c", t=4))
-            if ok(c + 1):
-                exps(c + 1)
             if ok(c - 1):
                 square_sum(dd[c - 1][:], sq, c - 1, "q")
-            small = ok(c) and c % 4 == 0
-            cols = slice(c, c + 4)
+            if ok(c + 1):
+                exps(c + 1)
+            if ok(c):
+                noise(c)
+            if ok(n) and on_vector(n):
+                exit_hx(n, nc.vector.tensor_copy)
+            if ok(n - 1):
+                add_mu(n - 1)
+                add_lv(n - 1)
+            if ok(n):
+                quant_hx(n)
+            if n == 1:
+                nc.vector.quantize_mx(out=wvbc[:].bitcast(FP8X4), scales=wvbs[:], in_=wvbg[:])
+            small = ok(c + 1) and (c + 1) % 4 == 0
+            cols = slice(c + 1, c + 5)
+            if ok(c):
+                sample(c)
+                resid(c)
             if small:
                 nc.vector.tensor_scalar(
                     out=sa[:, cols], in0=vx[:, cols], scalar1=BETA, scalar2=BETA * FLOOR, op0=ALU.mult, op1=ALU.add,
                 )
                 nc.vector.tensor_scalar_add(out=sm[:, cols], in0=vm[:, cols], scalar1=FLOOR)
-            if ok(n - 1):
-                add_mu(n - 1)
+            if ok(n - 2):
+                quant_mu(n - 2)
             if small:
                 nc.vector.reciprocal(out=sr[:, cols], in_=sm[:, cols])
                 nc.vector.tensor_tensor(out=sn[:, cols], in0=sa[:, cols], in1=sm[:, cols], op=ALU.min)
-            if ok(n - 1):
-                add_lv(n - 1)
-            if small:
-                nc.vector.tensor_tensor(out=sf[:, cols], in0=sn[:, cols], in1=sr[:, cols], op=ALU.mult)
-            if ok(c):
-                noise(c)
-            if ok(n):
-                quant_hx(n)
-            if n == 1:
-                nc.vector.quantize_mx(out=wvbc[:].bitcast(FP8X4), scales=wvbs[:], in_=wvbg[:])
-            if ok(c):
-                sample(c)
-                resid(c)
-            if ok(n - 2):
-                quant_mu(n - 2)
             if ok(c):
                 whiten(c)
-                if c % 2 == 1:
-                    nc.sync.dma_start(out=fv[:, 1024 * (c // 2) : 1024 * (c // 2 + 1)], in_=fxp[c // 2][:])
+            if small:
+                nc.vector.tensor_tensor(out=sf[:, cols], in0=sn[:, cols], in1=sr[:, cols], op=ALU.mult)
+            if ok(c) and c % 2 == 1:
+                nc.sync.dma_start(out=fv[:, 1024 * (c // 2) : 1024 * (c // 2 + 1)], in_=fxp[c // 2][:])
 
         lp = const.tile([P, NT], F32, name="lp")
         nc.vector.tensor_tensor(out=lp[:], in0=sl[:], in1=sq[:], op=ALU.add)

@@ -159,9 +159,9 @@ def tile_mdn_module_pa_t_kernel(tc, h, W2, b2, x, y, eps, Wv, out_0, out_1):
             umps[j] = psum.tile([P, 512], F32, name="umps%d" % j, tag="umps")
             mx(umps[j][:], cmu[j][:], smu[j][:], wvbc[:], wvbs[:])
 
-        def exit_hx(j, copy):
+        def exit_hx(j):
             grp[j] = work.tile([P, 1024], BF16, name="grp%d" % j, tag="grp", align_bytes=64)
-            copy(
+            nc.scalar.copy(
                 out=grp[j][:].bitcast(F32).rearrange("p (o r u) -> p o r u", o=2, u=2),
                 in_=tp[j][:].rearrange("p (o u r) -> p o r u", o=2, u=2),
             )
@@ -209,7 +209,7 @@ def tile_mdn_module_pa_t_kernel(tc, h, W2, b2, x, y, eps, Wv, out_0, out_1):
             if c % 2 == 0:
                 fxp[c // 2] = work.tile([P, 1024], F32, name="fx%d" % (c // 2), tag="fx", bufs=4)
             dst = fxp[c // 2][:, 512 * (c % 2) : 512 * (c % 2 + 1)]
-            nc.gpsimd.tensor_tensor(out=dst, in0=sd[c][:], in1=eq[q][:, 512 * i : 512 * (i + 1)], op=ALU.mult)
+            nc.vector.tensor_tensor(out=dst, in0=sd[c][:], in1=eq[q][:, 512 * i : 512 * (i + 1)], op=ALU.mult)
 
         def sample(c):
             dst = fxp[c // 2][:, 512 * (c % 2) : 512 * (c % 2 + 1)]
@@ -228,9 +228,6 @@ def tile_mdn_module_pa_t_kernel(tc, h, W2, b2, x, y, eps, Wv, out_0, out_1):
         def whiten(c):
             nc.vector.tensor_tensor(out=dd[c][:], in0=dd[c][:], in1=isd[c][:], op=ALU.mult)
 
-        def on_vector(j):
-            return j % 3 != 0
-
         for n in range(NT + LAG + 2):
             c = n - LAG
             if n % 4 == 0:
@@ -246,8 +243,8 @@ def tile_mdn_module_pa_t_kernel(tc, h, W2, b2, x, y, eps, Wv, out_0, out_1):
                 mx3(n - 1)
             if ok(n - 3):
                 mxu(n - 3)
-            if ok(n) and not on_vector(n):
-                exit_hx(n, nc.scalar.copy)
+            if ok(n):
+                exit_hx(n)
             if ok(n - 2):
                 exit_mu(n - 2)
             if ok(n - 1):
@@ -256,42 +253,41 @@ def tile_mdn_module_pa_t_kernel(tc, h, W2, b2, x, y, eps, Wv, out_0, out_1):
                 square_sum(umps[n - 3][:], vm, n - 3, "m")
             if n == 0:
                 regroup(nc.scalar.copy, wvbg[:], wvbraw[:].rearrange("p (t c) -> p t c", t=4))
-            if ok(c - 1):
-                square_sum(dd[c - 1][:], sq, c - 1, "q")
             if ok(c + 1):
                 exps(c + 1)
-            if ok(c):
-                noise(c)
-            if ok(n) and on_vector(n):
-                exit_hx(n, nc.vector.tensor_copy)
-            if ok(n - 1):
-                add_mu(n - 1)
-                add_lv(n - 1)
-            if ok(n):
-                quant_hx(n)
-            if n == 1:
-                nc.vector.quantize_mx(out=wvbc[:].bitcast(FP8X4), scales=wvbs[:], in_=wvbg[:])
-            small = ok(c + 1) and (c + 1) % 4 == 0
-            cols = slice(c + 1, c + 5)
-            if ok(c):
-                sample(c)
-                resid(c)
+            if ok(c - 1):
+                square_sum(dd[c - 1][:], sq, c - 1, "q")
+            small = ok(c) and c % 4 == 0
+            cols = slice(c, c + 4)
             if small:
                 nc.vector.tensor_scalar(
                     out=sa[:, cols], in0=vx[:, cols], scalar1=BETA, scalar2=BETA * FLOOR, op0=ALU.mult, op1=ALU.add,
                 )
                 nc.vector.tensor_scalar_add(out=sm[:, cols], in0=vm[:, cols], scalar1=FLOOR)
-            if ok(n - 2):
-                quant_mu(n - 2)
+            if ok(n - 1):
+                add_mu(n - 1)
             if small:
                 nc.vector.reciprocal(out=sr[:, cols], in_=sm[:, cols])
                 nc.vector.tensor_tensor(out=sn[:, cols], in0=sa[:, cols], in1=sm[:, cols], op=ALU.min)
-            if ok(c):
-                whiten(c)
+            if ok(n - 1):
+                add_lv(n - 1)
             if small:
                 nc.vector.tensor_tensor(out=sf[:, cols], in0=sn[:, cols], in1=sr[:, cols], op=ALU.mult)
-            if ok(c) and c % 2 == 1:
-                nc.sync.dma_start(out=fv[:, 1024 * (c // 2) : 1024 * (c // 2 + 1)], in_=fxp[c // 2][:])
+            if ok(c):
+                noise(c)
+            if ok(n):
+                quant_hx(n)
+            if n == 1:
+                nc.vector.quantize_mx(out=wvbc[:].bitcast(FP8X4), scales=wvbs[:], in_=wvbg[:])
+            if ok(c):
+                sample(c)
+                resid(c)
+            if ok(n - 2):
+                quant_mu(n - 2)
+            if ok(c):
+                whiten(c)
+                if c % 2 == 1:
+                    nc.sync.dma_start(out=fv[:, 1024 * (c // 2) : 1024 * (c // 2 + 1)], in_=fxp[c // 2][:])
 
         lp = const.tile([P, NT], F32, name="lp")
         nc.vector.tensor_tensor(out=lp[:], in0=sl[:], in1=sq[:], op=ALU.add)

@@ -21,7 +21,12 @@ BETA = 0.99
 FLOOR = 1e-3
 FLOPS = 2 * B * H * (2 * N) + 2 * 2 * B * N * N
 PIN = True
-LAG = 7
+AT_F = 2
+AT_T = 3
+AT_U = 4
+AT_EXP = 6
+AT_NOISE = 7
+LAG = 8
 
 
 def tile_mdn_module_pa_t_kernel(tc, h, W2, b2, x, y, eps, Wv, out_0, out_1):
@@ -42,10 +47,16 @@ def tile_mdn_module_pa_t_kernel(tc, h, W2, b2, x, y, eps, Wv, out_0, out_1):
         work = ctx.enter_context(tc.tile_pool(name="work", bufs=3))
         psum = ctx.enter_context(tc.psum_pool(name="psum", bufs=1))
 
-        w2raw = stage.tile([P, 4 * 1024], BF16, name="w2raw")
-        w2v = W2.rearrange("(u p e) c -> p u (e c)", u=2, p=P, e=2)
-        for u in range(2):
-            nc.sync.dma_start(out=w2raw[:, 2048 * u : 2048 * (u + 1)], in_=w2v[:, u, :])
+        w2v = W2.rearrange("(u p e) c -> p u e c", u=2, p=P, e=2)
+        w2raw = []
+        for half in range(2):
+            raw = stage.tile([P, 4 * 512], BF16, name="w2raw%d" % half)
+            for u in range(2):
+                nc.sync.dma_start(
+                    out=raw[:, 1024 * u : 1024 * (u + 1)].rearrange("p (e c) -> p e c", e=2),
+                    in_=w2v[:, u, :, 512 * half : 512 * (half + 1)],
+                )
+            w2raw.append(raw)
 
         hq, xq, yq, eq = {}, {}, {}, {}
 
@@ -62,13 +73,13 @@ def tile_mdn_module_pa_t_kernel(tc, h, W2, b2, x, y, eps, Wv, out_0, out_1):
             nc.sync.dma_start(out=yq[q][:], in_=yv[:, 2048 * q : 2048 * (q + 1)])
 
         load_hx(0)
+        bias = const.tile([P, 2 * N], BF16, name="bias")
+        nc.sync.dma_start(out=bias[:], in_=b2.partition_broadcast(P))
         wvaraw = stage.tile([P, 4 * 512], BF16, name="wvaraw")
         nc.sync.dma_start(
             out=wvaraw[:].rearrange("p (u f) -> p u f", u=2),
             in_=Wv.rearrange("(u p e) c -> p u (e c)", u=2, p=P, e=2),
         )
-        bias = const.tile([P, 2 * N], BF16, name="bias")
-        nc.sync.dma_start(out=bias[:], in_=b2.partition_broadcast(P))
         wvbraw = stage.tile([P, 4 * 512], BF16, name="wvbraw")
         nc.sync.dma_start(
             out=wvbraw[:].rearrange("p (t c) -> p t c", t=4),
@@ -98,12 +109,9 @@ def tile_mdn_module_pa_t_kernel(tc, h, W2, b2, x, y, eps, Wv, out_0, out_1):
                 in_=src.rearrange("p t (c i) -> p c t i", i=4),
             )
 
-        w2r3 = w2raw[:].rearrange("p (t c) -> p t c", t=4)
-        regroup(nc.vector.tensor_copy, w2g[:, 0:2048], w2r3[:, :, 0:512])
-        regroup(nc.scalar.copy, w2g[:, 2048:4096], w2r3[:, :, 512:1024])
-        regroup(nc.vector.tensor_copy, wvag[:], wvaraw[:].rearrange("p (t c) -> p t c", t=4))
+        regroup(nc.vector.tensor_copy, w2g[:, 0:2048], w2raw[0][:].rearrange("p (t c) -> p t c", t=4))
+        regroup(nc.scalar.copy, w2g[:, 2048:4096], w2raw[1][:].rearrange("p (t c) -> p t c", t=4))
         nc.vector.quantize_mx(out=w2c[:, 0:512].bitcast(FP8X4), scales=w2s[:, 0:512], in_=w2g[:, 0:2048])
-        nc.vector.quantize_mx(out=wvac[:].bitcast(FP8X4), scales=wvas[:], in_=wvag[:])
         nc.vector.quantize_mx(out=w2c[:, 512:1024].bitcast(FP8X4), scales=w2s[:, 512:1024], in_=w2g[:, 2048:4096])
 
         vx = const.tile([P, NT], F32, name="vx")
@@ -179,13 +187,13 @@ def tile_mdn_module_pa_t_kernel(tc, h, W2, b2, x, y, eps, Wv, out_0, out_1):
 
         def exps(j):
             sd[j] = work.tile([P, 512], F32, name="sd%d" % j, tag="sd")
-            isd[j] = work.tile([P, 512], F32, name="isd%d" % j, tag="isd")
+            isd[j] = work.tile([P, 512], F32, name="isd%d" % j, tag="isd", bufs=4)
             nc.scalar.activation(out=sd[j][:], in_=lv32[j][:], func=ACT.Exp, scale=0.5)
             nc.scalar.activation(out=isd[j][:], in_=lv32[j][:], func=ACT.Exp, scale=-0.5)
 
         def quant_hx(j):
-            cod[j] = work.tile([P, 256], U32, name="cod%d" % j, tag="cod", align_bytes=64)
-            scl[j] = work.tile([P, 256], U8, name="scl%d" % j, tag="scl", align_bytes=64)
+            cod[j] = work.tile([P, 256], U32, name="cod%d" % j, tag="cod", bufs=4, align_bytes=64)
+            scl[j] = work.tile([P, 256], U8, name="scl%d" % j, tag="scl", bufs=4, align_bytes=64)
             nc.vector.quantize_mx(out=cod[j][:].bitcast(FP8X4), scales=scl[j][:], in_=grp[j][:])
 
         def quant_mu(j):
@@ -194,11 +202,11 @@ def tile_mdn_module_pa_t_kernel(tc, h, W2, b2, x, y, eps, Wv, out_0, out_1):
             nc.vector.quantize_mx(out=cmu[j][:].bitcast(FP8X4), scales=smu[j][:], in_=gmu[j][:])
 
         def add_mu(j):
-            mu32[j] = work.tile([P, 512], F32, name="mu%d" % j, tag="mu32", bufs=LAG + 1)
+            mu32[j] = work.tile([P, 512], F32, name="mu%d" % j, tag="mu32", bufs=LAG + 2)
             nc.vector.tensor_tensor(out=mu32[j][:], in0=mups[j][:], in1=bias[:, 0:N], op=ALU.add)
 
         def add_lv(j):
-            lv32[j] = work.tile([P, 512], F32, name="lv%d" % j, tag="lv32", bufs=LAG + 1)
+            lv32[j] = work.tile([P, 512], F32, name="lv%d" % j, tag="lv32", bufs=AT_EXP)
             nc.vector.scalar_tensor_tensor(
                 out=lv32[j][:], in0=lvps[j][:], scalar=1.0, in1=bias[:, N : 2 * N],
                 op0=ALU.mult, op1=ALU.add, accum_out=sl[:, j : j + 1],
@@ -237,24 +245,22 @@ def tile_mdn_module_pa_t_kernel(tc, h, W2, b2, x, y, eps, Wv, out_0, out_1):
                     load_hx(n // 4 + 2)
             if ok(n):
                 t_hx(n)
-            if ok(n - 2):
-                t_mu(n - 2)
-            if ok(n - 1):
-                mx3(n - 1)
-            if ok(n - 3):
-                mxu(n - 3)
+            if ok(n - AT_T):
+                t_mu(n - AT_T)
+            if ok(n - AT_F):
+                mx3(n - AT_F)
+            if ok(n - AT_U):
+                mxu(n - AT_U)
             if ok(n):
                 exit_hx(n)
-            if ok(n - 2):
-                exit_mu(n - 2)
-            if ok(n - 1):
-                square_sum(uxps[n - 1][:], vx, n - 1, "x")
-            if ok(n - 3):
-                square_sum(umps[n - 3][:], vm, n - 3, "m")
-            if n == 0:
-                regroup(nc.scalar.copy, wvbg[:], wvbraw[:].rearrange("p (t c) -> p t c", t=4))
-            if ok(c + 1):
-                exps(c + 1)
+            if ok(n - AT_T):
+                exit_mu(n - AT_T)
+            if ok(n - AT_F):
+                square_sum(uxps[n - AT_F][:], vx, n - AT_F, "x")
+            if ok(n - AT_U):
+                square_sum(umps[n - AT_U][:], vm, n - AT_U, "m")
+            if ok(n - AT_EXP):
+                exps(n - AT_EXP)
             if ok(c - 1):
                 square_sum(dd[c - 1][:], sq, c - 1, "q")
             small = ok(c) and c % 4 == 0
@@ -264,26 +270,31 @@ def tile_mdn_module_pa_t_kernel(tc, h, W2, b2, x, y, eps, Wv, out_0, out_1):
                     out=sa[:, cols], in0=vx[:, cols], scalar1=BETA, scalar2=BETA * FLOOR, op0=ALU.mult, op1=ALU.add,
                 )
                 nc.vector.tensor_scalar_add(out=sm[:, cols], in0=vm[:, cols], scalar1=FLOOR)
-            if ok(n - 1):
-                add_mu(n - 1)
+            if ok(n - AT_F):
+                add_mu(n - AT_F)
             if small:
                 nc.vector.reciprocal(out=sr[:, cols], in_=sm[:, cols])
                 nc.vector.tensor_tensor(out=sn[:, cols], in0=sa[:, cols], in1=sm[:, cols], op=ALU.min)
-            if ok(n - 1):
-                add_lv(n - 1)
+            if ok(n - AT_F):
+                add_lv(n - AT_F)
             if small:
                 nc.vector.tensor_tensor(out=sf[:, cols], in0=sn[:, cols], in1=sr[:, cols], op=ALU.mult)
-            if ok(c):
-                noise(c)
             if ok(n):
                 quant_hx(n)
+            if n == 0:
+                regroup(nc.vector.tensor_copy, wvag[:], wvaraw[:].rearrange("p (t c) -> p t c", t=4))
+                nc.vector.quantize_mx(out=wvac[:].bitcast(FP8X4), scales=wvas[:], in_=wvag[:])
             if n == 1:
+                regroup(nc.vector.tensor_copy, wvbg[:], wvbraw[:].rearrange("p (t c) -> p t c", t=4))
+            if n == 2:
                 nc.vector.quantize_mx(out=wvbc[:].bitcast(FP8X4), scales=wvbs[:], in_=wvbg[:])
             if ok(c):
-                sample(c)
                 resid(c)
-            if ok(n - 2):
-                quant_mu(n - 2)
+                sample(c)
+            if ok(n - AT_T):
+                quant_mu(n - AT_T)
+            if ok(n - AT_NOISE):
+                noise(n - AT_NOISE)
             if ok(c):
                 whiten(c)
                 if c % 2 == 1:

@@ -1,9 +1,7 @@
 from contextlib import ExitStack
 import math
 
-import concourse.bass as bass
 import concourse.mybir as mybir
-import concourse.tile as tile
 from concourse.masks import make_identity
 
 F32 = mybir.dt.float32
@@ -13,20 +11,17 @@ U8 = mybir.dt.uint8
 FP8X4 = mybir.dt.float8_e4m3fn_x4
 ALU = mybir.AluOpType
 ACT = mybir.ActivationFunctionType
+AX = mybir.AxisListType
 
 P = 128
 B, N, H = 4096, 512, 512
 NT = B // P
+NP = NT // 2
+W = 2 * P
 BETA = 0.99
 FLOOR = 1e-3
 FLOPS = 2 * B * H * (2 * N) + 2 * 2 * B * N * N
-PIN = True
-AT_F = 2
-AT_T = 3
-AT_U = 4
-AT_EXP = 6
-AT_NOISE = 7
-LAG = 8
+LAG = 5
 
 
 def tile_mdn_module_pa_t_kernel(tc, h, W2, b2, x, y, eps, Wv, out_0, out_1):
@@ -39,13 +34,29 @@ def tile_mdn_module_pa_t_kernel(tc, h, W2, b2, x, y, eps, Wv, out_0, out_1):
     lv = out_1.rearrange("(p j) o -> p (j o)", j=NT)
 
     with ExitStack() as ctx:
-        if PIN:
-            ctx.enter_context(tc.manual_schedule())
+        ctx.enter_context(tc.manual_schedule())
         const = ctx.enter_context(tc.tile_pool(name="const", bufs=1))
         stage = ctx.enter_context(tc.tile_pool(name="stage", bufs=1))
         loads = ctx.enter_context(tc.tile_pool(name="loads", bufs=3))
         work = ctx.enter_context(tc.tile_pool(name="work", bufs=3))
         psum = ctx.enter_context(tc.psum_pool(name="psum", bufs=1))
+
+        hq, xq, yq, eq = {}, {}, {}, {}
+
+        def load_hx(q, parts):
+            hq[q] = loads.tile([P, 2048], BF16, name="hq%d" % q, tag="hq")
+            xq[q] = loads.tile([P, 2048], BF16, name="xq%d" % q, tag="xq")
+            w = 2048 // parts
+            for s in range(parts):
+                lo, hi = w * s, w * (s + 1)
+                nc.sync.dma_start(out=hq[q][:, lo:hi], in_=hv[:, 2048 * q + lo : 2048 * q + hi])
+                nc.sync.dma_start(out=xq[q][:, lo:hi], in_=xv[:, 2048 * q + lo : 2048 * q + hi])
+
+        def load_ye(q):
+            eq[q] = loads.tile([P, 2048], BF16, name="eq%d" % q, tag="eq")
+            nc.sync.dma_start(out=eq[q][:], in_=ev[:, 2048 * q : 2048 * (q + 1)])
+            yq[q] = loads.tile([P, 2048], BF16, name="yq%d" % q, tag="yq")
+            nc.sync.dma_start(out=yq[q][:], in_=yv[:, 2048 * q : 2048 * (q + 1)])
 
         w2v = W2.rearrange("(u p e) c -> p u e c", u=2, p=P, e=2)
         w2raw = []
@@ -57,252 +68,323 @@ def tile_mdn_module_pa_t_kernel(tc, h, W2, b2, x, y, eps, Wv, out_0, out_1):
                     in_=w2v[:, u, :, 512 * half : 512 * (half + 1)],
                 )
             w2raw.append(raw)
-
-        hq, xq, yq, eq = {}, {}, {}, {}
-
-        def load_hx(q):
-            hq[q] = loads.tile([P, 2048], BF16, name="hq%d" % q, tag="hq")
-            nc.sync.dma_start(out=hq[q][:], in_=hv[:, 2048 * q : 2048 * (q + 1)])
-            xq[q] = loads.tile([P, 2048], BF16, name="xq%d" % q, tag="xq")
-            nc.sync.dma_start(out=xq[q][:], in_=xv[:, 2048 * q : 2048 * (q + 1)])
-
-        def load_ye(q):
-            eq[q] = loads.tile([P, 2048], BF16, name="eq%d" % q, tag="eq")
-            nc.sync.dma_start(out=eq[q][:], in_=ev[:, 2048 * q : 2048 * (q + 1)])
-            yq[q] = loads.tile([P, 2048], BF16, name="yq%d" % q, tag="yq")
-            nc.sync.dma_start(out=yq[q][:], in_=yv[:, 2048 * q : 2048 * (q + 1)])
-
-        load_hx(0)
-        bias = const.tile([P, 2 * N], BF16, name="bias")
-        nc.sync.dma_start(out=bias[:], in_=b2.partition_broadcast(P))
-        wvaraw = stage.tile([P, 4 * 512], BF16, name="wvaraw")
-        nc.sync.dma_start(
-            out=wvaraw[:].rearrange("p (u f) -> p u f", u=2),
-            in_=Wv.rearrange("(u p e) c -> p u (e c)", u=2, p=P, e=2),
-        )
-        wvbraw = stage.tile([P, 4 * 512], BF16, name="wvbraw")
-        nc.sync.dma_start(
-            out=wvbraw[:].rearrange("p (t c) -> p t c", t=4),
-            in_=Wv.rearrange("(t p) c -> p t c", p=P),
-        )
-        load_hx(1)
+            if half == 0:
+                load_hx(0, 2)
+                bb = const.tile([P, 8], BF16, name="bb")
+                nc.sync.dma_start(
+                    out=bb[:].rearrange("p (o t) -> p o t", o=2), in_=b2.rearrange("(o p t) -> p o t", o=2, t=4)
+                )
+        wvraw = stage.tile([P, 4 * 512], BF16, name="wvraw")
+        nc.sync.dma_start(out=wvraw[:], in_=Wv.rearrange("(p t) c -> p (t c)", t=4))
+        load_hx(1, 1)
 
         ident = const.tile([P, P], F32, name="ident")
         make_identity(nc, ident[:])
+        ones = const.tile([P, P], BF16, name="ones")
+        nc.gpsimd.memset(ones[:], 1.0)
         warm = const.tile([P, 1], F32, name="warm")
         nc.vector.memset(warm[:], 0.0)
         nc.scalar.activation(out=warm[:], in_=warm[:], func=ACT.Exp)
 
         w2c = const.tile([P, 1024], U32, name="w2c", align_bytes=64)
         w2s = const.tile([P, 1024], U8, name="w2s", align_bytes=64)
-        wvac = const.tile([P, 512], U32, name="wvac", align_bytes=64)
-        wvas = const.tile([P, 512], U8, name="wvas", align_bytes=64)
-        wvbc = const.tile([P, 512], U32, name="wvbc", align_bytes=64)
-        wvbs = const.tile([P, 512], U8, name="wvbs", align_bytes=64)
+        wvc = const.tile([P, 512], U32, name="wvc", align_bytes=64)
+        wvs = const.tile([P, 512], U8, name="wvs", align_bytes=64)
         w2g = stage.tile([P, 4096], BF16, name="w2g", align_bytes=64)
-        wvag = stage.tile([P, 2048], BF16, name="wvag", align_bytes=64)
-        wvbg = stage.tile([P, 2048], BF16, name="wvbg", align_bytes=64)
+        wvg = stage.tile([P, 2048], BF16, name="wvg", align_bytes=64)
 
-        def regroup(copy, dst, src):
+        def regroup_channels(copy, dst, src):
             copy(
-                out=dst.rearrange("p (c i t) -> p c t i", i=4, t=4),
-                in_=src.rearrange("p t (c i) -> p c t i", i=4),
+                out=dst.rearrange("p (t m j) -> p t m j", t=4, j=4),
+                in_=src.rearrange("p (j m t) -> p t m j", j=4, t=4),
             )
 
-        regroup(nc.vector.tensor_copy, w2g[:, 0:2048], w2raw[0][:].rearrange("p (t c) -> p t c", t=4))
-        regroup(nc.scalar.copy, w2g[:, 2048:4096], w2raw[1][:].rearrange("p (t c) -> p t c", t=4))
+        def gpsimd_copy(out, in_):
+            nc.gpsimd.tensor_scalar(out=out, in0=in_, scalar1=1.0, scalar2=0.0, op0=ALU.mult, op1=ALU.add)
+
+        regroup_channels(nc.vector.tensor_copy, w2g[:, 0:2048], w2raw[0][:])
         nc.vector.quantize_mx(out=w2c[:, 0:512].bitcast(FP8X4), scales=w2s[:, 0:512], in_=w2g[:, 0:2048])
-        nc.vector.quantize_mx(out=w2c[:, 512:1024].bitcast(FP8X4), scales=w2s[:, 512:1024], in_=w2g[:, 2048:4096])
+
+        regroup_channels(gpsimd_copy, w2g[:, 2048:4096], w2raw[1][:])
+
+        bf32 = const.tile([P, 8], F32, name="bf32")
+        nc.vector.tensor_copy(out=bf32[:], in_=bb[:])
+        bpos = const.tile([P, 4], F32, name="bpos")
+        nc.vector.tensor_scalar_mul(out=bpos[:], in0=bb[:, 4:8], scalar1=0.5)
+        bneg = const.tile([P, 4], F32, name="bneg")
+        nc.vector.tensor_scalar_mul(out=bneg[:], in0=bb[:, 4:8], scalar1=-0.5)
 
         vx = const.tile([P, NT], F32, name="vx")
         vm = const.tile([P, NT], F32, name="vm")
         sq = const.tile([P, NT], F32, name="sq")
         sl = const.tile([P, NT], F32, name="sl")
-        sa = const.tile([P, NT], F32, name="sa")
         sm = const.tile([P, NT], F32, name="sm")
         sr = const.tile([P, NT], F32, name="sr")
         sn = const.tile([P, NT], F32, name="sn")
         sf = const.tile([P, NT], F32, name="sf")
 
-        tp, grp, cod, scl = {}, {}, {}, {}
-        mups, lvps, uxps, umps, mtps = {}, {}, {}, {}, {}
-        mu32, lv32, gmu, cmu, smu = {}, {}, {}, {}, {}
-        sd, isd, dd, fxp = {}, {}, {}, {}
+        btot = const.tile([P, 1], F32, name="btot")
+        base = const.tile([P, 1], F32, name="base")
 
-        def ok(j):
+        tp, grp, cod, scl = {}, {}, {}, {}
+        mz, ub, sgb, sdb, mub, isb = {}, {}, {}, {}, {}, {}
+        mut, sdt, ist, gmu, cmu, smu = {}, {}, {}, {}, {}, {}
+        dd, fxp = {}, {}
+
+        def okt(j):
             return 0 <= j < NT
+
+        def okp(p):
+            return 0 <= p < NP
 
         def t_hx(j):
             q, i = divmod(j, 4)
-            tp[j] = psum.tile([P, 512], F32, name="tp%d" % j, tag="tp", bufs=2)
-            for o, src in enumerate((hq[q], xq[q])):
-                words = src[:].bitcast(F32)
-                for u in range(2):
-                    nc.tensor.transpose(
-                        tp[j][:, (2 * o + u) * P : (2 * o + u + 1) * P],
-                        words[:, 256 * i + P * u : 256 * i + P * (u + 1)],
-                        ident[:],
-                    )
+            tp[j] = psum.tile([P, 512], F32, name="tp%d" % j, tag="tp")
+            hw = hq[q][:].bitcast(F32)
+            xw = xq[q][:].bitcast(F32)
+            for u in range(2):
+                nc.tensor.transpose(
+                    tp[j][:, u * P : (u + 1) * P], hw[:, 256 * i + P * u : 256 * i + P * (u + 1)], ident[:]
+                )
+            for u in range(2):
+                nc.tensor.transpose(
+                    tp[j][:, (2 + u) * P : (3 + u) * P], xw[:, 256 * i + u : 256 * (i + 1) : 2], ident[:]
+                )
 
-        def t_mu(j):
-            mtps[j] = psum.tile([P, 512], F32, name="mt%d" % j, tag="mt", bufs=2)
+        def t_back(store, src, c, label):
+            p, a = divmod(c, 2)
+            store[c] = psum.tile([P, 512], F32, name="%s%d" % (label, c), tag=label)
             for t in range(4):
-                nc.tensor.transpose(mtps[j][:, P * t : P * (t + 1)], mu32[j][:, P * t : P * (t + 1)], ident[:])
+                nc.tensor.transpose(
+                    store[c][:, P * t : P * (t + 1)], src[p][:, W * t + P * a : W * t + P * (a + 1)], ident[:]
+                )
 
-        def mx(out, lc, ls, rc, rs):
+        def mx(out, lc, ls, rc, rs, start=True, stop=True):
             nc.tensor.matmul_mx(
                 out=out, lhsT=lc.bitcast(FP8X4), lhsT_scale=ls, rhs=rc.bitcast(FP8X4), rhs_scale=rs,
-                start=True, stop=True,
+                start=start, stop=stop,
             )
 
-        def mx3(j):
-            mups[j] = psum.tile([P, 512], F32, name="mups%d" % j, tag="mups")
-            lvps[j] = psum.tile([P, 512], F32, name="lvps%d" % j, tag="lvps")
-            uxps[j] = psum.tile([P, 512], F32, name="uxps%d" % j, tag="uxps")
-            mx(mups[j][:], cod[j][:, 0:P], scl[j][:, 0:P], w2c[:, 0:512], w2s[:, 0:512])
-            mx(lvps[j][:], cod[j][:, 0:P], scl[j][:, 0:P], w2c[:, 512:1024], w2s[:, 512:1024])
-            mx(uxps[j][:], cod[j][:, P : 2 * P], scl[j][:, P : 2 * P], wvac[:], wvas[:])
+        def m_chan(p, base):
+            for b in range(2):
+                t0 = psum.tile([P, 512], F32, name="mz%d_%d_%d" % (p, base, b), tag="mz", bufs=2)
+                mz[p, base, b] = t0
+                for e in range(2):
+                    col = base + P * (2 * b + e)
+                    mx(t0[:, W * e : W * (e + 1)], w2c[:, col : col + P], w2s[:, col : col + P],
+                       cod[p][:, 0:W], scl[p][:, 0:W])
 
-        def mxu(j):
-            umps[j] = psum.tile([P, 512], F32, name="umps%d" % j, tag="umps")
-            mx(umps[j][:], cmu[j][:], smu[j][:], wvbc[:], wvbs[:])
+        def m_u(key, lc, ls):
+            t0 = psum.tile([P, 512], F32, name="u_%s_%d" % key, tag="u", bufs=2)
+            ub[key] = t0
+            mx(t0[:], lc, ls, wvc[:], wvs[:])
 
-        def exit_hx(j):
-            grp[j] = work.tile([P, 1024], BF16, name="grp%d" % j, tag="grp", align_bytes=64)
-            nc.scalar.copy(
-                out=grp[j][:].bitcast(F32).rearrange("p (o r u) -> p o r u", o=2, u=2),
-                in_=tp[j][:].rearrange("p (o u r) -> p o r u", o=2, u=2),
-            )
+        def m_ux(j):
+            p, a = divmod(j, 2)
+            cols = slice(W + P * a, W + P * (a + 1))
+            m_u(("x", j), cod[p][:, cols], scl[p][:, cols])
 
-        def exit_mu(j):
-            gmu[j] = work.tile([P, 512], BF16, name="gmu%d" % j, tag="gmu", align_bytes=64)
-            nc.scalar.copy(
-                out=gmu[j][:].rearrange("p (r t) -> p r t", t=4),
-                in_=mtps[j][:].rearrange("p (t r) -> p r t", t=4),
-            )
+        def m_um(j):
+            p, a = divmod(j, 2)
+            cols = slice(P * a, P * (a + 1))
+            m_u(("m", j), cmu[p][:, cols], smu[p][:, cols])
+
+        def m_sum(p):
+            sgb[p] = psum.tile([P, 512], F32, name="sg%d" % p, tag="u", bufs=2)
+            for a in range(2):
+                rows = slice(P * a, P * (a + 1))
+                for t in range(4):
+                    cols = slice(512 + P * t, 512 + P * (t + 1))
+                    mx(sgb[p][:, rows], cod[p][:, rows], scl[p][:, rows], w2c[:, cols], w2s[:, cols],
+                       start=(t == 0), stop=(t == 3))
 
         def square_sum(src, acc, j, label):
             junk = work.tile([P, 512], BF16, name="junk%s%d" % (label, j), tag="junk", bufs=2)
             nc.scalar.activation(out=junk[:], in_=src, func=ACT.Square, accum_out=acc[:, j : j + 1])
 
-        def exps(j):
-            sd[j] = work.tile([P, 512], F32, name="sd%d" % j, tag="sd")
-            isd[j] = work.tile([P, 512], F32, name="isd%d" % j, tag="isd", bufs=4)
-            nc.scalar.activation(out=sd[j][:], in_=lv32[j][:], func=ACT.Exp, scale=0.5)
-            nc.scalar.activation(out=isd[j][:], in_=lv32[j][:], func=ACT.Exp, scale=-0.5)
+        def s_mu(p):
+            mut[p] = work.tile([P, 1024], F32, name="mut%d" % p, tag="mut", bufs=4)
+            for t in range(4):
+                nc.scalar.activation(
+                    out=mut[p][:, W * t : W * (t + 1)], in_=mz[p, 0, t // 2][:, W * (t % 2) : W * (t % 2 + 1)],
+                    func=ACT.Identity, bias=bf32[:, t : t + 1],
+                )
 
-        def quant_hx(j):
-            cod[j] = work.tile([P, 256], U32, name="cod%d" % j, tag="cod", bufs=4, align_bytes=64)
-            scl[j] = work.tile([P, 256], U8, name="scl%d" % j, tag="scl", bufs=4, align_bytes=64)
-            nc.vector.quantize_mx(out=cod[j][:].bitcast(FP8X4), scales=scl[j][:], in_=grp[j][:])
+        def s_exp(p):
+            sdt[p] = work.tile([P, 1024], F32, name="sdt%d" % p, tag="sdt", bufs=4)
+            ist[p] = work.tile([P, 1024], F32, name="ist%d" % p, tag="ist", bufs=4)
+            for t in range(4):
+                src = mz[p, 512, t // 2][:, W * (t % 2) : W * (t % 2 + 1)]
+                cols = slice(W * t, W * (t + 1))
+                nc.scalar.activation(out=sdt[p][:, cols], in_=src, func=ACT.Exp, bias=bpos[:, t : t + 1], scale=0.5)
+                nc.scalar.activation(out=ist[p][:, cols], in_=src, func=ACT.Exp, bias=bneg[:, t : t + 1], scale=-0.5)
 
-        def quant_mu(j):
-            cmu[j] = work.tile([P, P], U32, name="cmu%d" % j, tag="cmu", align_bytes=64)
-            smu[j] = work.tile([P, P], U8, name="smu%d" % j, tag="smu", align_bytes=64)
-            nc.vector.quantize_mx(out=cmu[j][:].bitcast(FP8X4), scales=smu[j][:], in_=gmu[j][:])
-
-        def add_mu(j):
-            mu32[j] = work.tile([P, 512], F32, name="mu%d" % j, tag="mu32", bufs=LAG + 2)
-            nc.vector.tensor_tensor(out=mu32[j][:], in0=mups[j][:], in1=bias[:, 0:N], op=ALU.add)
-
-        def add_lv(j):
-            lv32[j] = work.tile([P, 512], F32, name="lv%d" % j, tag="lv32", bufs=AT_EXP)
-            nc.vector.scalar_tensor_tensor(
-                out=lv32[j][:], in0=lvps[j][:], scalar=1.0, in1=bias[:, N : 2 * N],
-                op0=ALU.mult, op1=ALU.add, accum_out=sl[:, j : j + 1],
+        def exit_hx(j):
+            p, a = divmod(j, 2)
+            if a == 0:
+                grp[p] = work.tile([P, 2048], BF16, name="grp%d" % p, tag="grp", align_bytes=64)
+            copy = nc.scalar.copy if j < 2 else nc.vector.tensor_copy
+            copy(
+                out=grp[p][:].bitcast(F32).rearrange("p (o a r u) -> p o a r u", o=2, a=2, u=2)[:, :, a],
+                in_=tp[j][:].rearrange("p (o u r) -> p o r u", o=2, u=2),
             )
+
+        def quant_hx(p):
+            cod[p] = work.tile([P, 512], U32, name="cod%d" % p, tag="cod", align_bytes=64)
+            scl[p] = work.tile([P, 512], U8, name="scl%d" % p, tag="scl", align_bytes=64)
+            nc.vector.quantize_mx(out=cod[p][:].bitcast(FP8X4), scales=scl[p][:], in_=grp[p][:])
+
+        def quant_mu(p):
+            cmu[p] = work.tile([P, W], U32, name="cmu%d" % p, tag="cmu", align_bytes=64)
+            smu[p] = work.tile([P, W], U8, name="smu%d" % p, tag="smu", align_bytes=64)
+            nc.vector.quantize_mx(out=cmu[p][:].bitcast(FP8X4), scales=smu[p][:], in_=gmu[p][:])
+
+        def reduce_lv(p):
+            nc.vector.tensor_reduce(
+                out=sl[:, 2 * p : 2 * p + 2], in_=sgb[p][:, 0:W].rearrange("p (a m) -> p a m", a=2), axis=AX.X, op=ALU.add
+            )
+
+        def tm(bank):
+            return bank[:].rearrange("p (t m) -> p m t", t=4)
+
+        def mt(ap):
+            return ap.rearrange("p (m t) -> p m t", t=4)
+
+        def fx_of(c):
+            return mt(fxp[c // 2][:, 512 * (c % 2) : 512 * (c % 2 + 1)])
 
         def noise(c):
             q, i = divmod(c, 4)
             if c % 2 == 0:
-                fxp[c // 2] = work.tile([P, 1024], F32, name="fx%d" % (c // 2), tag="fx", bufs=4)
-            dst = fxp[c // 2][:, 512 * (c % 2) : 512 * (c % 2 + 1)]
-            nc.vector.tensor_tensor(out=dst, in0=sd[c][:], in1=eq[q][:, 512 * i : 512 * (i + 1)], op=ALU.mult)
-
-        def sample(c):
-            dst = fxp[c // 2][:, 512 * (c % 2) : 512 * (c % 2 + 1)]
-            nc.vector.scalar_tensor_tensor(
-                out=dst, in0=mu32[c][:], scalar=sf[:, c : c + 1], in1=dst, op0=ALU.mult, op1=ALU.add,
+                fxp[c // 2] = work.tile([P, 1024], F32, name="fx%d" % (c // 2), tag="fx")
+            nc.vector.tensor_tensor(
+                out=fx_of(c), in0=tm(sdb[c]), in1=mt(eq[q][:, 512 * i : 512 * (i + 1)]), op=ALU.mult
             )
 
         def resid(c):
             q, i = divmod(c, 4)
             dd[c] = work.tile([P, 512], F32, name="dd%d" % c, tag="dd")
             nc.vector.scalar_tensor_tensor(
-                out=dd[c][:], in0=mu32[c][:], scalar=sf[:, c : c + 1], in1=yq[q][:, 512 * i : 512 * (i + 1)],
+                out=mt(dd[c][:]), in0=tm(mub[c]), scalar=sf[:, c : c + 1], in1=mt(yq[q][:, 512 * i : 512 * (i + 1)]),
                 op0=ALU.mult, op1=ALU.subtract,
             )
 
-        def whiten(c):
-            nc.vector.tensor_tensor(out=dd[c][:], in0=dd[c][:], in1=isd[c][:], op=ALU.mult)
+        def sample(c):
+            nc.vector.scalar_tensor_tensor(
+                out=fx_of(c), in0=tm(mub[c]), scalar=sf[:, c : c + 1], in1=fx_of(c), op0=ALU.mult, op1=ALU.add
+            )
+            if c % 2 == 1:
+                nc.sync.dma_start(out=fv[:, 1024 * (c // 2) : 1024 * (c // 2 + 1)], in_=fxp[c // 2][:])
 
-        for n in range(NT + LAG + 2):
-            c = n - LAG
-            if n % 4 == 0:
-                if n // 4 < NT // 4:
-                    load_ye(n // 4)
-                if n // 4 + 2 < NT // 4:
-                    load_hx(n // 4 + 2)
-            if ok(n):
-                t_hx(n)
-            if ok(n - AT_T):
-                t_mu(n - AT_T)
-            if ok(n - AT_F):
-                mx3(n - AT_F)
-            if ok(n - AT_U):
-                mxu(n - AT_U)
-            if ok(n):
-                exit_hx(n)
-            if ok(n - AT_T):
-                exit_mu(n - AT_T)
-            if ok(n - AT_F):
-                square_sum(uxps[n - AT_F][:], vx, n - AT_F, "x")
-            if ok(n - AT_U):
-                square_sum(umps[n - AT_U][:], vm, n - AT_U, "m")
-            if ok(n - AT_EXP):
-                exps(n - AT_EXP)
-            if ok(c - 1):
-                square_sum(dd[c - 1][:], sq, c - 1, "q")
-            small = ok(c) and c % 4 == 0
-            cols = slice(c, c + 4)
-            if small:
-                nc.vector.tensor_scalar(
-                    out=sa[:, cols], in0=vx[:, cols], scalar1=BETA, scalar2=BETA * FLOOR, op0=ALU.mult, op1=ALU.add,
-                )
-                nc.vector.tensor_scalar_add(out=sm[:, cols], in0=vm[:, cols], scalar1=FLOOR)
-            if ok(n - AT_F):
-                add_mu(n - AT_F)
-            if small:
-                nc.vector.reciprocal(out=sr[:, cols], in_=sm[:, cols])
-                nc.vector.tensor_tensor(out=sn[:, cols], in0=sa[:, cols], in1=sm[:, cols], op=ALU.min)
-            if ok(n - AT_F):
-                add_lv(n - AT_F)
-            if small:
-                nc.vector.tensor_tensor(out=sf[:, cols], in0=sn[:, cols], in1=sr[:, cols], op=ALU.mult)
-            if ok(n):
-                quant_hx(n)
-            if n == 0:
-                regroup(nc.vector.tensor_copy, wvag[:], wvaraw[:].rearrange("p (t c) -> p t c", t=4))
-                nc.vector.quantize_mx(out=wvac[:].bitcast(FP8X4), scales=wvas[:], in_=wvag[:])
-            if n == 1:
-                regroup(nc.vector.tensor_copy, wvbg[:], wvbraw[:].rearrange("p (t c) -> p t c", t=4))
-            if n == 2:
-                nc.vector.quantize_mx(out=wvbc[:].bitcast(FP8X4), scales=wvbs[:], in_=wvbg[:])
-            if ok(c):
-                resid(c)
-                sample(c)
-            if ok(n - AT_T):
-                quant_mu(n - AT_T)
-            if ok(n - AT_NOISE):
-                noise(n - AT_NOISE)
-            if ok(c):
-                whiten(c)
-                if c % 2 == 1:
-                    nc.sync.dma_start(out=fv[:, 1024 * (c // 2) : 1024 * (c // 2 + 1)], in_=fxp[c // 2][:])
+        def whiten(c):
+            nc.vector.tensor_tensor(out=mt(dd[c][:]), in0=mt(dd[c][:]), in1=tm(isb[c]), op=ALU.mult)
+
+        def group_mu(p):
+            gmu[p] = work.tile([P, 1024], BF16, name="gmu%d" % p, tag="gmu", align_bytes=64)
+            nc.gpsimd.tensor_scalar(
+                out=gmu[p][:].rearrange("p (r t) -> p r t", t=4), in0=mut[p][:].rearrange("p (t r) -> p r t", t=4),
+                scalar1=1.0, scalar2=0.0, op0=ALU.mult, op1=ALU.add,
+            )
+
+        t_hx(0)
+        for i in range(NT + LAG + 1):
+            n, half = divmod(i, 2)
+            c = i - LAG
+            new, old = n - 1, n - 2
+            if i % 4 == 0:
+                if i // 4 < NT // 4:
+                    load_ye(i // 4)
+                if i // 4 + 2 < NT // 4:
+                    load_hx(i // 4 + 2, 1)
+            if half == 0:
+                cols = slice(2 * old, 2 * old + 2)
+                if okt(c):
+                    noise(c)
+                if okp(new):
+                    quant_hx(new)
+                if i == 2:
+                    nc.vector.tensor_copy(
+                        out=wvg[:].rearrange("p (c k t) -> p c t k", k=4, t=4),
+                        in_=wvraw[:].rearrange("p (t c k) -> p c t k", t=4, k=4),
+                    )
+                    nc.vector.quantize_mx(out=wvc[:].bitcast(FP8X4), scales=wvs[:], in_=wvg[:])
+                if okp(old):
+                    m_um(2 * old)
+                    m_um(2 * old + 1)
+                if okp(new):
+                    m_chan(new, 0)
+                    m_ux(2 * new)
+                if okp(old):
+                    square_sum(ub["m", 2 * old][:], vm, 2 * old, "m")
+                    square_sum(ub["m", 2 * old + 1][:], vm, 2 * old + 1, "m")
+                if okt(c - 1):
+                    square_sum(dd[c - 1][:], sq, c - 1, "q")
+                if okp(new):
+                    s_mu(new)
+                    square_sum(ub["x", 2 * new][:], vx, 2 * new, "x")
+                    group_mu(new)
+                if okt(c):
+                    resid(c)
+                if okp(old):
+                    nc.vector.tensor_scalar_add(out=sm[:, cols], in0=vm[:, cols], scalar1=FLOOR)
+                if okt(c):
+                    sample(c)
+                if okp(old):
+                    nc.vector.reciprocal(out=sr[:, cols], in_=sm[:, cols])
+                if okt(c):
+                    whiten(c)
+                if okp(old):
+                    nc.vector.scalar_tensor_tensor(
+                        out=sn[:, cols], in0=vx[:, cols], scalar=FLOOR, in1=sr[:, cols], op0=ALU.add, op1=ALU.mult
+                    )
+                if okt(i):
+                    exit_hx(i)
+                if i == 2:
+                    nc.vector.quantize_mx(
+                        out=w2c[:, 512:1024].bitcast(FP8X4), scales=w2s[:, 512:1024], in_=w2g[:, 2048:4096]
+                    )
+                if i == 4:
+                    bsum = psum.tile([P, 512], F32, name="bsum", tag="u", bufs=2)
+                    nc.tensor.matmul(bsum[:, 0:4], lhsT=ones[:], rhs=bb[:, 4:8], start=True, stop=True)
+                    nc.vector.tensor_reduce(out=btot[:], in_=bsum[:, 0:4], axis=AX.X, op=ALU.add)
+                    nc.vector.tensor_scalar(
+                        out=base[:], in0=btot[:], scalar1=-0.5, scalar2=-0.5 * N * math.log(2.0 * math.pi),
+                        op0=ALU.mult, op1=ALU.add,
+                    )
+                if okp(old):
+                    nc.vector.tensor_scalar(
+                        out=sf[:, cols], in0=sn[:, cols], scalar1=BETA, scalar2=1.0, op0=ALU.mult, op1=ALU.min
+                    )
+            else:
+                if okp(new):
+                    m_chan(new, 512)
+                    m_sum(new)
+                    m_ux(2 * new + 1)
+                if okt(c - 1):
+                    square_sum(dd[c - 1][:], sq, c - 1, "q")
+                if okp(new):
+                    s_exp(new)
+                    square_sum(ub["x", 2 * new + 1][:], vx, 2 * new + 1, "x")
+                if okt(c):
+                    noise(c)
+                    resid(c)
+                    sample(c)
+                    whiten(c)
+                if okt(i):
+                    exit_hx(i)
+                if okp(new):
+                    reduce_lv(new)
+                    quant_mu(new)
+            if okt(c + 1):
+                t_back(sdb, sdt, c + 1, "sd")
+                t_back(mub, mut, c + 1, "mu")
+                t_back(isb, ist, c + 1, "is")
+            if okt(i + 1):
+                t_hx(i + 1)
 
         lp = const.tile([P, NT], F32, name="lp")
         nc.vector.tensor_tensor(out=lp[:], in0=sl[:], in1=sq[:], op=ALU.add)
         nc.vector.tensor_scalar(
-            out=lp[:], in0=lp[:], scalar1=-0.5, scalar2=-0.5 * N * math.log(2.0 * math.pi), op0=ALU.mult, op1=ALU.add,
+            out=lp[:], in0=lp[:], scalar1=-0.5, scalar2=base[:, 0:1], op0=ALU.mult, op1=ALU.add
         )
         nc.sync.dma_start(out=lv, in_=lp[:])

@@ -70,12 +70,12 @@ def tile_mdn_module_pa_t_kernel(tc, h, W2, b2, x, y, eps, Wv, out_0, out_1):
             w2raw.append(raw)
             if half == 0:
                 load_hx(0, 2)
-                bb = const.tile([P, 8], BF16, name="bb")
-                nc.sync.dma_start(
-                    out=bb[:].rearrange("p (o t) -> p o t", o=2), in_=b2.rearrange("(o p t) -> p o t", o=2, t=4)
-                )
+                bm = const.tile([P, 4], BF16, name="bm")
+                nc.sync.dma_start(out=bm[:], in_=b2[0:N].rearrange("(p t) -> p t", t=4))
         wvraw = stage.tile([P, 4 * 512], BF16, name="wvraw")
         nc.sync.dma_start(out=wvraw[:], in_=Wv.rearrange("(p t) c -> p (t c)", t=4))
+        bl = const.tile([P, 4], BF16, name="bl")
+        nc.sync.dma_start(out=bl[:], in_=b2[N : 2 * N].rearrange("(t p) -> p t", p=P))
         load_hx(1, 1)
 
         ident = const.tile([P, P], F32, name="ident")
@@ -93,26 +93,24 @@ def tile_mdn_module_pa_t_kernel(tc, h, W2, b2, x, y, eps, Wv, out_0, out_1):
         w2g = stage.tile([P, 4096], BF16, name="w2g", align_bytes=64)
         wvg = stage.tile([P, 2048], BF16, name="wvg", align_bytes=64)
 
-        def regroup_channels(copy, dst, src):
+        def regroup(copy, dst, src):
             copy(
-                out=dst.rearrange("p (t m j) -> p t m j", t=4, j=4),
-                in_=src.rearrange("p (j m t) -> p t m j", j=4, t=4),
+                out=dst.rearrange("p (c k j) -> p c j k", k=4, j=4),
+                in_=src.rearrange("p j (c k) -> p c j k", k=4),
             )
 
-        def gpsimd_copy(out, in_):
-            nc.gpsimd.tensor_scalar(out=out, in0=in_, scalar1=1.0, scalar2=0.0, op0=ALU.mult, op1=ALU.add)
 
-        regroup_channels(nc.vector.tensor_copy, w2g[:, 0:2048], w2raw[0][:])
+        nc.vector.tensor_copy(
+            out=w2g[:, 0:2048].rearrange("p (t m j) -> p t m j", t=4, j=4),
+            in_=w2raw[0][:].rearrange("p (j m t) -> p t m j", j=4, t=4),
+        )
         nc.vector.quantize_mx(out=w2c[:, 0:512].bitcast(FP8X4), scales=w2s[:, 0:512], in_=w2g[:, 0:2048])
 
-        regroup_channels(gpsimd_copy, w2g[:, 2048:4096], w2raw[1][:])
 
-        bf32 = const.tile([P, 8], F32, name="bf32")
-        nc.vector.tensor_copy(out=bf32[:], in_=bb[:])
+        bf32 = const.tile([P, 4], F32, name="bf32")
+        nc.vector.tensor_copy(out=bf32[:], in_=bm[:])
         bpos = const.tile([P, 4], F32, name="bpos")
-        nc.vector.tensor_scalar_mul(out=bpos[:], in0=bb[:, 4:8], scalar1=0.5)
         bneg = const.tile([P, 4], F32, name="bneg")
-        nc.vector.tensor_scalar_mul(out=bneg[:], in0=bb[:, 4:8], scalar1=-0.5)
 
         vx = const.tile([P, NT], F32, name="vx")
         vm = const.tile([P, NT], F32, name="vm")
@@ -169,6 +167,8 @@ def tile_mdn_module_pa_t_kernel(tc, h, W2, b2, x, y, eps, Wv, out_0, out_1):
             for b in range(2):
                 t0 = psum.tile([P, 512], F32, name="mz%d_%d_%d" % (p, base, b), tag="mz", bufs=2)
                 mz[p, base, b] = t0
+                if b < 1 and base == 0:
+                    nc.tensor.matmul(t0[:], lhsT=ones[:], rhs=w2g[:, 0:512], start=True, stop=True)
                 for e in range(2):
                     col = base + P * (2 * b + e)
                     mx(t0[:, W * e : W * (e + 1)], w2c[:, col : col + P], w2s[:, col : col + P],
@@ -210,14 +210,20 @@ def tile_mdn_module_pa_t_kernel(tc, h, W2, b2, x, y, eps, Wv, out_0, out_1):
                     func=ACT.Identity, bias=bf32[:, t : t + 1],
                 )
 
-        def s_exp(p):
-            sdt[p] = work.tile([P, 1024], F32, name="sdt%d" % p, tag="sdt", bufs=4)
-            ist[p] = work.tile([P, 1024], F32, name="ist%d" % p, tag="ist", bufs=4)
-            for t in range(4):
-                src = mz[p, 512, t // 2][:, W * (t % 2) : W * (t % 2 + 1)]
-                cols = slice(W * t, W * (t + 1))
-                nc.scalar.activation(out=sdt[p][:, cols], in_=src, func=ACT.Exp, bias=bpos[:, t : t + 1], scale=0.5)
-                nc.scalar.activation(out=ist[p][:, cols], in_=src, func=ACT.Exp, bias=bneg[:, t : t + 1], scale=-0.5)
+        def s_exp(p, bank, store, label, bias, scale):
+            if bank == 0:
+                store[p] = work.tile([P, 1024], F32, name="%s%d" % (label, p), tag=label, bufs=4)
+            for t in (2 * bank, 2 * bank + 1):
+                nc.scalar.activation(
+                    out=store[p][:, W * t : W * (t + 1)], in_=mz[p, 512, bank][:, W * (t % 2) : W * (t % 2 + 1)],
+                    func=ACT.Exp, bias=bias[:, t : t + 1], scale=scale,
+                )
+
+        def s_sd(p, bank):
+            s_exp(p, bank, sdt, "sdt", bpos, 0.5)
+
+        def s_is(p, bank):
+            s_exp(p, bank, ist, "ist", bneg, -0.5)
 
         def exit_hx(j):
             p, a = divmod(j, 2)
@@ -258,7 +264,8 @@ def tile_mdn_module_pa_t_kernel(tc, h, W2, b2, x, y, eps, Wv, out_0, out_1):
             if c % 2 == 0:
                 fxp[c // 2] = work.tile([P, 1024], F32, name="fx%d" % (c // 2), tag="fx")
             nc.vector.tensor_tensor(
-                out=fx_of(c), in0=tm(sdb[c]), in1=mt(eq[q][:, 512 * i : 512 * (i + 1)]), op=ALU.mult
+                out=fxp[c // 2][:, 512 * (c % 2) : 512 * (c % 2 + 1)], in0=sdb[c][:],
+                in1=eq[q][:, 512 * i : 512 * (i + 1)], op=ALU.mult,
             )
 
         def resid(c):
@@ -277,110 +284,140 @@ def tile_mdn_module_pa_t_kernel(tc, h, W2, b2, x, y, eps, Wv, out_0, out_1):
                 nc.sync.dma_start(out=fv[:, 1024 * (c // 2) : 1024 * (c // 2 + 1)], in_=fxp[c // 2][:])
 
         def whiten(c):
-            nc.vector.tensor_tensor(out=mt(dd[c][:]), in0=mt(dd[c][:]), in1=tm(isb[c]), op=ALU.mult)
+            nc.vector.tensor_tensor(out=dd[c][:], in0=dd[c][:], in1=isb[c][:], op=ALU.mult)
 
         def group_mu(p):
             gmu[p] = work.tile([P, 1024], BF16, name="gmu%d" % p, tag="gmu", align_bytes=64)
-            nc.gpsimd.tensor_scalar(
-                out=gmu[p][:].rearrange("p (r t) -> p r t", t=4), in0=mut[p][:].rearrange("p (t r) -> p r t", t=4),
-                scalar1=1.0, scalar2=0.0, op0=ALU.mult, op1=ALU.add,
+            out = gmu[p][:].rearrange("p (r t) -> p r t", t=4)
+            src = mut[p][:].rearrange("p (t r) -> p r t", t=4)
+            if p == 0:
+                nc.vector.tensor_copy(out=out, in_=src)
+            else:
+                nc.gpsimd.tensor_scalar(out=out, in0=src, scalar1=1.0, scalar2=0.0, op0=ALU.mult, op1=ALU.add)
+
+        def prepare_wv():
+            regroup(nc.vector.tensor_copy, wvg[:], wvraw[:].rearrange("p (j c) -> p j c", j=4))
+            nc.vector.quantize_mx(out=wvc[:].bitcast(FP8X4), scales=wvs[:], in_=wvg[:])
+
+        def quant_lv():
+            nc.vector.tensor_scalar_mul(out=bpos[:], in0=bl[:], scalar1=0.5)
+            nc.vector.tensor_scalar_mul(out=bneg[:], in0=bl[:], scalar1=-0.5)
+            nc.vector.quantize_mx(out=w2c[:, 512:1024].bitcast(FP8X4), scales=w2s[:, 512:1024], in_=w2g[:, 2048:4096])
+
+        def bias_sum():
+            bsum = psum.tile([P, 512], F32, name="bsum", tag="u", bufs=2)
+            nc.tensor.matmul(bsum[:, 0:4], lhsT=ones[:], rhs=bl[:], start=True, stop=True)
+            nc.vector.tensor_reduce(out=btot[:], in_=bsum[:, 0:4], axis=AX.X, op=ALU.add)
+            nc.vector.tensor_scalar(
+                out=base[:], in0=btot[:], scalar1=-0.5, scalar2=-0.5 * N * math.log(2.0 * math.pi),
+                op0=ALU.mult, op1=ALU.add,
+            )
+
+        def pair_cols(p):
+            return slice(2 * p, 2 * p + 2)
+
+        def factor_a(p):
+            nc.vector.tensor_scalar_add(out=sm[:, pair_cols(p)], in0=vm[:, pair_cols(p)], scalar1=FLOOR)
+
+        def factor_b(p):
+            nc.vector.reciprocal(out=sr[:, pair_cols(p)], in_=sm[:, pair_cols(p)])
+
+        def factor_c(p):
+            nc.vector.tensor_scalar(
+                out=sn[:, pair_cols(p)], in0=vx[:, pair_cols(p)], scalar1=FLOOR, scalar2=BETA, op0=ALU.add, op1=ALU.mult
+            )
+
+        def factor_d(j):
+            nc.vector.tensor_scalar(
+                out=sf[:, j : j + 1], in0=sn[:, j : j + 1], scalar1=sr[:, j : j + 1], scalar2=1.0,
+                op0=ALU.mult, op1=ALU.min,
             )
 
         t_hx(0)
-        for i in range(NT + LAG + 1):
-            n, half = divmod(i, 2)
-            c = i - LAG
-            new, old = n - 1, n - 2
-            if i % 4 == 0:
-                if i // 4 < NT // 4:
-                    load_ye(i // 4)
-                if i // 4 + 2 < NT // 4:
-                    load_hx(i // 4 + 2, 1)
-            if half == 0:
-                cols = slice(2 * old, 2 * old + 2)
-                if okt(c):
-                    noise(c)
-                if okp(new):
-                    quant_hx(new)
-                if i == 2:
-                    nc.vector.tensor_copy(
-                        out=wvg[:].rearrange("p (c k t) -> p c t k", k=4, t=4),
-                        in_=wvraw[:].rearrange("p (t c k) -> p c t k", t=4, k=4),
-                    )
-                    nc.vector.quantize_mx(out=wvc[:].bitcast(FP8X4), scales=wvs[:], in_=wvg[:])
-                if okp(old):
-                    m_um(2 * old)
-                    m_um(2 * old + 1)
-                if okp(new):
-                    m_chan(new, 0)
-                    m_ux(2 * new)
-                if okp(old):
-                    square_sum(ub["m", 2 * old][:], vm, 2 * old, "m")
-                    square_sum(ub["m", 2 * old + 1][:], vm, 2 * old + 1, "m")
-                if okt(c - 1):
-                    square_sum(dd[c - 1][:], sq, c - 1, "q")
-                if okp(new):
-                    s_mu(new)
-                    square_sum(ub["x", 2 * new][:], vx, 2 * new, "x")
-                    group_mu(new)
-                if okt(c):
-                    resid(c)
-                if okp(old):
-                    nc.vector.tensor_scalar_add(out=sm[:, cols], in0=vm[:, cols], scalar1=FLOOR)
-                if okt(c):
-                    sample(c)
-                if okp(old):
-                    nc.vector.reciprocal(out=sr[:, cols], in_=sm[:, cols])
-                if okt(c):
-                    whiten(c)
-                if okp(old):
-                    nc.vector.scalar_tensor_tensor(
-                        out=sn[:, cols], in0=vx[:, cols], scalar=FLOOR, in1=sr[:, cols], op0=ALU.add, op1=ALU.mult
-                    )
-                if okt(i):
-                    exit_hx(i)
-                if i == 2:
-                    nc.vector.quantize_mx(
-                        out=w2c[:, 512:1024].bitcast(FP8X4), scales=w2s[:, 512:1024], in_=w2g[:, 2048:4096]
-                    )
-                if i == 4:
-                    bsum = psum.tile([P, 512], F32, name="bsum", tag="u", bufs=2)
-                    nc.tensor.matmul(bsum[:, 0:4], lhsT=ones[:], rhs=bb[:, 4:8], start=True, stop=True)
-                    nc.vector.tensor_reduce(out=btot[:], in_=bsum[:, 0:4], axis=AX.X, op=ALU.add)
-                    nc.vector.tensor_scalar(
-                        out=base[:], in0=btot[:], scalar1=-0.5, scalar2=-0.5 * N * math.log(2.0 * math.pi),
-                        op0=ALU.mult, op1=ALU.add,
-                    )
-                if okp(old):
-                    nc.vector.tensor_scalar(
-                        out=sf[:, cols], in0=sn[:, cols], scalar1=BETA, scalar2=1.0, op0=ALU.mult, op1=ALU.min
-                    )
-            else:
-                if okp(new):
-                    m_chan(new, 512)
-                    m_sum(new)
-                    m_ux(2 * new + 1)
-                if okt(c - 1):
-                    square_sum(dd[c - 1][:], sq, c - 1, "q")
-                if okp(new):
-                    s_exp(new)
-                    square_sum(ub["x", 2 * new + 1][:], vx, 2 * new + 1, "x")
-                if okt(c):
-                    noise(c)
-                    resid(c)
-                    sample(c)
-                    whiten(c)
-                if okt(i):
-                    exit_hx(i)
-                if okp(new):
-                    reduce_lv(new)
-                    quant_mu(new)
-            if okt(c + 1):
-                t_back(sdb, sdt, c + 1, "sd")
-                t_back(mub, mut, c + 1, "mu")
-                t_back(isb, ist, c + 1, "is")
-            if okt(i + 1):
-                t_hx(i + 1)
+        for n in range(NP + 3):
+            front, new, old = n, n - 1, n - 2
+            if n % 2 == 0:
+                if n // 2 < NT // 4:
+                    load_ye(n // 2)
+                if n // 2 + 2 < NT // 4:
+                    load_hx(n // 2 + 2, 1)
+            if okp(new):
+                quant_hx(new)
+            if n == 1:
+                half = w2raw[1][:].rearrange("p (j c) -> p j c", j=4)
+                regroup(nc.vector.tensor_copy, w2g[:, 2048:3072], half[:, :, 0:256])
+                regroup(nc.scalar.copy, w2g[:, 3072:4096], half[:, :, 256:512])
+                prepare_wv()
+                quant_lv()
+            if okp(old):
+                square_sum(ub["x", 2 * old + 1][:], vx, 2 * old + 1, "x")
+            if okt(2 * old - 1):
+                square_sum(dd[2 * old - 1][:], sq, 2 * old - 1, "q")
+            if okp(old):
+                t_back(mub, mut, 2 * old, "mu")
+                t_back(isb, ist, 2 * old, "is")
+            if okp(new):
+                m_chan(new, 0)
+                m_ux(2 * new)
+            if okp(old):
+                factor_b(old)
+            if okp(front):
+                exit_hx(2 * front)
+            if n == 2:
+                bias_sum()
+            if okp(old):
+                factor_c(old)
+                noise(2 * old)
+                factor_d(2 * old)
+                factor_d(2 * old + 1)
+            if okp(new):
+                s_mu(new)
+                group_mu(new)
+                square_sum(ub["x", 2 * new][:], vx, 2 * new, "x")
+            if okp(new):
+                m_chan(new, 512)
+            if okp(old):
+                resid(2 * old)
+                sample(2 * old)
+                whiten(2 * old)
+            if okp(new):
+                s_sd(new, 0)
+                s_is(new, 0)
+            if okp(old):
+                t_back(sdb, sdt, 2 * old + 1, "sd")
+                t_back(mub, mut, 2 * old + 1, "mu")
+            if okp(front):
+                t_hx(2 * front + 1)
+            if okp(old):
+                noise(2 * old + 1)
+                square_sum(dd[2 * old][:], sq, 2 * old, "q")
+            if okp(new):
+                quant_mu(new)
+                m_sum(new)
+                m_um(2 * new)
+                m_um(2 * new + 1)
+                s_sd(new, 1)
+            if okp(old):
+                resid(2 * old + 1)
+            if okp(front):
+                exit_hx(2 * front + 1)
+            if okp(old):
+                sample(2 * old + 1)
+                t_back(isb, ist, 2 * old + 1, "is")
+            if okp(new):
+                t_back(sdb, sdt, 2 * new, "sd")
+            if okp(front + 1):
+                t_hx(2 * front + 2)
+            if okp(new):
+                square_sum(ub["m", 2 * new][:], vm, 2 * new, "m")
+                square_sum(ub["m", 2 * new + 1][:], vm, 2 * new + 1, "m")
+                reduce_lv(new)
+            if okp(old):
+                whiten(2 * old + 1)
+            if okp(new):
+                s_is(new, 1)
+                factor_a(new)
+                m_ux(2 * new + 1)
 
         lp = const.tile([P, NT], F32, name="lp")
         nc.vector.tensor_tensor(out=lp[:], in0=sl[:], in1=sq[:], op=ALU.add)

@@ -21,7 +21,7 @@ W = 2 * P
 BETA = 0.99
 FLOOR = 1e-3
 FLOPS = 2 * B * H * (2 * N) + 2 * 2 * B * N * N
-LAG = 5
+V_BLOCK = 3
 
 
 def tile_mdn_module_pa_t_kernel(tc, h, W2, b2, x, y, eps, Wv, out_0, out_1):
@@ -74,14 +74,12 @@ def tile_mdn_module_pa_t_kernel(tc, h, W2, b2, x, y, eps, Wv, out_0, out_1):
                 nc.sync.dma_start(out=bm[:], in_=b2[0:N].rearrange("(p t) -> p t", t=4))
         wvraw = stage.tile([P, 4 * 512], BF16, name="wvraw")
         nc.sync.dma_start(out=wvraw[:], in_=Wv.rearrange("(p t) c -> p (t c)", t=4))
-        bl = const.tile([P, 4], BF16, name="bl")
-        nc.sync.dma_start(out=bl[:], in_=b2[N : 2 * N].rearrange("(t p) -> p t", p=P))
+        bl = const.tile([P, N], BF16, name="bl")
+        nc.sync.dma_start(out=bl[:], in_=b2[N : 2 * N].partition_broadcast(P))
         load_hx(1, 1)
 
         ident = const.tile([P, P], F32, name="ident")
         make_identity(nc, ident[:])
-        ones = const.tile([P, P], BF16, name="ones")
-        nc.gpsimd.memset(ones[:], 1.0)
         warm = const.tile([P, 1], F32, name="warm")
         nc.vector.memset(warm[:], 0.0)
         nc.scalar.activation(out=warm[:], in_=warm[:], func=ACT.Exp)
@@ -109,8 +107,6 @@ def tile_mdn_module_pa_t_kernel(tc, h, W2, b2, x, y, eps, Wv, out_0, out_1):
 
         bf32 = const.tile([P, 4], F32, name="bf32")
         nc.vector.tensor_copy(out=bf32[:], in_=bm[:])
-        bpos = const.tile([P, 4], F32, name="bpos")
-        bneg = const.tile([P, 4], F32, name="bneg")
 
         vx = const.tile([P, NT], F32, name="vx")
         vm = const.tile([P, NT], F32, name="vm")
@@ -121,13 +117,10 @@ def tile_mdn_module_pa_t_kernel(tc, h, W2, b2, x, y, eps, Wv, out_0, out_1):
         sn = const.tile([P, NT], F32, name="sn")
         sf = const.tile([P, NT], F32, name="sf")
 
-        btot = const.tile([P, 1], F32, name="btot")
-        base = const.tile([P, 1], F32, name="base")
-
         tp, grp, cod, scl = {}, {}, {}, {}
-        mz, ub, sgb, sdb, mub, isb = {}, {}, {}, {}, {}, {}
-        mut, sdt, ist, gmu, cmu, smu = {}, {}, {}, {}, {}, {}
-        dd, fxp = {}, {}
+        mz, ub, lvb, mub = {}, {}, {}, {}
+        mut, gmu, cmu, smu = {}, {}, {}, {}
+        lv32, sd, isd, dd, fxp = {}, {}, {}, {}, {}
 
         def okt(j):
             return 0 <= j < NT
@@ -149,12 +142,12 @@ def tile_mdn_module_pa_t_kernel(tc, h, W2, b2, x, y, eps, Wv, out_0, out_1):
                     tp[j][:, (2 + u) * P : (3 + u) * P], xw[:, 256 * i + u : 256 * (i + 1) : 2], ident[:]
                 )
 
-        def t_back(store, src, c, label):
+        def t_mu(c):
             p, a = divmod(c, 2)
-            store[c] = psum.tile([P, 512], F32, name="%s%d" % (label, c), tag=label)
+            mub[c] = psum.tile([P, 512], F32, name="mub%d" % c, tag="mub", bufs=2)
             for t in range(4):
                 nc.tensor.transpose(
-                    store[c][:, P * t : P * (t + 1)], src[p][:, W * t + P * a : W * t + P * (a + 1)], ident[:]
+                    mub[c][:, P * t : P * (t + 1)], mut[p][:, W * t + P * a : W * t + P * (a + 1)], ident[:]
                 )
 
         def mx(out, lc, ls, rc, rs, start=True, stop=True):
@@ -163,67 +156,56 @@ def tile_mdn_module_pa_t_kernel(tc, h, W2, b2, x, y, eps, Wv, out_0, out_1):
                 start=start, stop=stop,
             )
 
-        def m_chan(p, base):
-            for b in range(2):
-                t0 = psum.tile([P, 512], F32, name="mz%d_%d_%d" % (p, base, b), tag="mz", bufs=2)
-                mz[p, base, b] = t0
-                if b < 1 and base == 0:
-                    nc.tensor.matmul(t0[:], lhsT=ones[:], rhs=w2g[:, 0:512], start=True, stop=True)
-                for e in range(2):
-                    col = base + P * (2 * b + e)
-                    mx(t0[:, W * e : W * (e + 1)], w2c[:, col : col + P], w2s[:, col : col + P],
-                       cod[p][:, 0:W], scl[p][:, 0:W])
+        def m_mu(p, b):
+            mz[p, b] = psum.tile([P, 512], F32, name="mz%d_%d" % (p, b), tag="mz")
+            if b == 0:
+                for d in range(1):
+                    nc.tensor.matmul(mz[p, b][:], lhsT=w2g[:, 0:P], rhs=w2g[:, 0:512], start=True, stop=True)
+            for e in range(2):
+                cols = slice(P * (2 * b + e), P * (2 * b + e + 1))
+                mx(mz[p, b][:, W * e : W * (e + 1)], w2c[:, cols], w2s[:, cols], cod[p][:, 0:W], scl[p][:, 0:W])
 
-        def m_u(key, lc, ls):
+        def m_u(key, lc, ls, keep=0):
             t0 = psum.tile([P, 512], F32, name="u_%s_%d" % key, tag="u", bufs=2)
             ub[key] = t0
+            for d in range(keep):
+                nc.tensor.matmul(t0[:], lhsT=w2g[:, 0:P], rhs=w2g[:, 0:512], start=True, stop=True)
             mx(t0[:], lc, ls, wvc[:], wvs[:])
 
         def m_ux(j):
             p, a = divmod(j, 2)
             cols = slice(W + P * a, W + P * (a + 1))
-            m_u(("x", j), cod[p][:, cols], scl[p][:, cols])
+            m_u(("x", j), cod[p][:, cols], scl[p][:, cols], 1 * a)
 
         def m_um(j):
             p, a = divmod(j, 2)
             cols = slice(P * a, P * (a + 1))
             m_u(("m", j), cmu[p][:, cols], smu[p][:, cols])
 
-        def m_sum(p):
-            sgb[p] = psum.tile([P, 512], F32, name="sg%d" % p, tag="u", bufs=2)
-            for a in range(2):
-                rows = slice(P * a, P * (a + 1))
-                for t in range(4):
-                    cols = slice(512 + P * t, 512 + P * (t + 1))
-                    mx(sgb[p][:, rows], cod[p][:, rows], scl[p][:, rows], w2c[:, cols], w2s[:, cols],
-                       start=(t == 0), stop=(t == 3))
+        def m_lv(j):
+            p, a = divmod(j, 2)
+            rows = slice(P * a, P * (a + 1))
+            lvb[j] = psum.tile([P, 512], F32, name="lvb%d" % j, tag="lv", bufs=2)
+            mx(lvb[j][:], cod[p][:, rows], scl[p][:, rows], w2c[:, 512:1024], w2s[:, 512:1024])
 
         def square_sum(src, acc, j, label):
             junk = work.tile([P, 512], BF16, name="junk%s%d" % (label, j), tag="junk", bufs=2)
             nc.scalar.activation(out=junk[:], in_=src, func=ACT.Square, accum_out=acc[:, j : j + 1])
 
-        def s_mu(p):
-            mut[p] = work.tile([P, 1024], F32, name="mut%d" % p, tag="mut", bufs=4)
-            for t in range(4):
-                nc.scalar.activation(
-                    out=mut[p][:, W * t : W * (t + 1)], in_=mz[p, 0, t // 2][:, W * (t % 2) : W * (t % 2 + 1)],
-                    func=ACT.Identity, bias=bf32[:, t : t + 1],
-                )
+        def mu_bias(p, t):
+            if t == 0:
+                mut[p] = work.tile([P, 1024], F32, name="mut%d" % p, tag="mut", bufs=4)
+            dst, src = mut[p][:, W * t : W * (t + 1)], mz[p, t // 2][:, W * (t % 2) : W * (t % 2 + 1)]
+            if t == V_BLOCK:
+                nc.vector.tensor_scalar_add(out=dst, in0=src, scalar1=bf32[:, t : t + 1])
+            else:
+                nc.scalar.activation(out=dst, in_=src, func=ACT.Identity, bias=bf32[:, t : t + 1])
 
-        def s_exp(p, bank, store, label, bias, scale):
-            if bank == 0:
-                store[p] = work.tile([P, 1024], F32, name="%s%d" % (label, p), tag=label, bufs=4)
-            for t in (2 * bank, 2 * bank + 1):
-                nc.scalar.activation(
-                    out=store[p][:, W * t : W * (t + 1)], in_=mz[p, 512, bank][:, W * (t % 2) : W * (t % 2 + 1)],
-                    func=ACT.Exp, bias=bias[:, t : t + 1], scale=scale,
-                )
-
-        def s_sd(p, bank):
-            s_exp(p, bank, sdt, "sdt", bpos, 0.5)
-
-        def s_is(p, bank):
-            s_exp(p, bank, ist, "ist", bneg, -0.5)
+        def exps(p):
+            sd[p] = work.tile([P, 1024], F32, name="sd%d" % p, tag="sd")
+            isd[p] = work.tile([P, 1024], F32, name="isd%d" % p, tag="isd")
+            nc.scalar.activation(out=sd[p][:], in_=lv32[p][:], func=ACT.Exp, scale=0.5)
+            nc.scalar.activation(out=isd[p][:], in_=lv32[p][:], func=ACT.Exp, scale=-0.5)
 
         def exit_hx(j):
             p, a = divmod(j, 2)
@@ -245,9 +227,13 @@ def tile_mdn_module_pa_t_kernel(tc, h, W2, b2, x, y, eps, Wv, out_0, out_1):
             smu[p] = work.tile([P, W], U8, name="smu%d" % p, tag="smu", align_bytes=64)
             nc.vector.quantize_mx(out=cmu[p][:].bitcast(FP8X4), scales=smu[p][:], in_=gmu[p][:])
 
-        def reduce_lv(p):
-            nc.vector.tensor_reduce(
-                out=sl[:, 2 * p : 2 * p + 2], in_=sgb[p][:, 0:W].rearrange("p (a m) -> p a m", a=2), axis=AX.X, op=ALU.add
+        def add_lv(j):
+            p, a = divmod(j, 2)
+            if a == 0:
+                lv32[p] = work.tile([P, 1024], F32, name="lv%d" % p, tag="lv32")
+            nc.vector.scalar_tensor_tensor(
+                out=lv32[p][:, 512 * a : 512 * (a + 1)], in0=lvb[j][:], scalar=1.0, in1=bl[:], op0=ALU.mult, op1=ALU.add,
+                accum_out=sl[:, j : j + 1],
             )
 
         def tm(bank):
@@ -259,18 +245,9 @@ def tile_mdn_module_pa_t_kernel(tc, h, W2, b2, x, y, eps, Wv, out_0, out_1):
         def fx_of(c):
             return mt(fxp[c // 2][:, 512 * (c % 2) : 512 * (c % 2 + 1)])
 
-        def noise(c):
-            q, i = divmod(c, 4)
-            if c % 2 == 0:
-                fxp[c // 2] = work.tile([P, 1024], F32, name="fx%d" % (c // 2), tag="fx")
-            nc.vector.tensor_tensor(
-                out=fxp[c // 2][:, 512 * (c % 2) : 512 * (c % 2 + 1)], in0=sdb[c][:],
-                in1=eq[q][:, 512 * i : 512 * (i + 1)], op=ALU.mult,
-            )
-
         def resid(c):
             q, i = divmod(c, 4)
-            dd[c] = work.tile([P, 512], F32, name="dd%d" % c, tag="dd")
+            dd[c] = work.tile([P, 512], F32, name="dd%d" % c, tag="dd", bufs=4)
             nc.vector.scalar_tensor_tensor(
                 out=mt(dd[c][:]), in0=tm(mub[c]), scalar=sf[:, c : c + 1], in1=mt(yq[q][:, 512 * i : 512 * (i + 1)]),
                 op0=ALU.mult, op1=ALU.subtract,
@@ -283,35 +260,31 @@ def tile_mdn_module_pa_t_kernel(tc, h, W2, b2, x, y, eps, Wv, out_0, out_1):
             if c % 2 == 1:
                 nc.sync.dma_start(out=fv[:, 1024 * (c // 2) : 1024 * (c // 2 + 1)], in_=fxp[c // 2][:])
 
-        def whiten(c):
-            nc.vector.tensor_tensor(out=dd[c][:], in0=dd[c][:], in1=isb[c][:], op=ALU.mult)
-
         def group_mu(p):
             gmu[p] = work.tile([P, 1024], BF16, name="gmu%d" % p, tag="gmu", align_bytes=64)
-            out = gmu[p][:].rearrange("p (r t) -> p r t", t=4)
-            src = mut[p][:].rearrange("p (t r) -> p r t", t=4)
-            if p == 0:
-                nc.vector.tensor_copy(out=out, in_=src)
-            else:
-                nc.gpsimd.tensor_scalar(out=out, in0=src, scalar1=1.0, scalar2=0.0, op0=ALU.mult, op1=ALU.add)
+            nc.vector.tensor_copy(
+                out=gmu[p][:].rearrange("p (r t) -> p r t", t=4), in_=mut[p][:].rearrange("p (t r) -> p r t", t=4)
+            )
+
+        def noise(p):
+            q, i = divmod(p, 2)
+            fxp[p] = work.tile([P, 1024], F32, name="fx%d" % p, tag="fx")
+            nc.gpsimd.tensor_tensor(
+                out=fxp[p][:], in0=sd[p][:], in1=eq[q][:, 1024 * i : 1024 * (i + 1)], op=ALU.mult
+            )
+
+        def whiten(c):
+            p, a = divmod(c, 2)
+            nc.gpsimd.tensor_tensor(
+                out=dd[c][:], in0=dd[c][:], in1=isd[p][:, 512 * a : 512 * (a + 1)], op=ALU.mult
+            )
 
         def prepare_wv():
             regroup(nc.vector.tensor_copy, wvg[:], wvraw[:].rearrange("p (j c) -> p j c", j=4))
             nc.vector.quantize_mx(out=wvc[:].bitcast(FP8X4), scales=wvs[:], in_=wvg[:])
 
         def quant_lv():
-            nc.vector.tensor_scalar_mul(out=bpos[:], in0=bl[:], scalar1=0.5)
-            nc.vector.tensor_scalar_mul(out=bneg[:], in0=bl[:], scalar1=-0.5)
             nc.vector.quantize_mx(out=w2c[:, 512:1024].bitcast(FP8X4), scales=w2s[:, 512:1024], in_=w2g[:, 2048:4096])
-
-        def bias_sum():
-            bsum = psum.tile([P, 512], F32, name="bsum", tag="u", bufs=2)
-            nc.tensor.matmul(bsum[:, 0:4], lhsT=ones[:], rhs=bl[:], start=True, stop=True)
-            nc.vector.tensor_reduce(out=btot[:], in_=bsum[:, 0:4], axis=AX.X, op=ALU.add)
-            nc.vector.tensor_scalar(
-                out=base[:], in0=btot[:], scalar1=-0.5, scalar2=-0.5 * N * math.log(2.0 * math.pi),
-                op0=ALU.mult, op1=ALU.add,
-            )
 
         def pair_cols(p):
             return slice(2 * p, 2 * p + 2)
@@ -334,94 +307,89 @@ def tile_mdn_module_pa_t_kernel(tc, h, W2, b2, x, y, eps, Wv, out_0, out_1):
             )
 
         t_hx(0)
-        for n in range(NP + 3):
-            front, new, old = n, n - 1, n - 2
+        exit_hx(0)
+        t_hx(1)
+        for n in range(NP + 4):
+            front, p0, p1, old = n, n - 1, n - 2, n - 3
+            a, b = 2 * old, 2 * old + 1
             if n % 2 == 0:
                 if n // 2 < NT // 4:
                     load_ye(n // 2)
                 if n // 2 + 2 < NT // 4:
                     load_hx(n // 2 + 2, 1)
-            if okp(new):
-                quant_hx(new)
+            if okp(old):
+                factor_a(old)
+                factor_c(old)
+            if okp(p1):
+                group_mu(p1)
+            if okp(old):
+                factor_b(old)
+            if okp(p0):
+                quant_hx(p0)
             if n == 1:
                 half = w2raw[1][:].rearrange("p (j c) -> p j c", j=4)
                 regroup(nc.vector.tensor_copy, w2g[:, 2048:3072], half[:, :, 0:256])
                 regroup(nc.scalar.copy, w2g[:, 3072:4096], half[:, :, 256:512])
                 prepare_wv()
                 quant_lv()
+            if okp(p1):
+                exps(p1)
+            if okt(a - 1):
+                square_sum(dd[a - 1][:], sq, a - 1, "q")
+            if okp(p0):
+                m_mu(p0, 0)
+                m_lv(2 * p0)
+                m_lv(2 * p0 + 1)
+                mu_bias(p0, 0)
+                mu_bias(p0, 1)
             if okp(old):
-                square_sum(ub["x", 2 * old + 1][:], vx, 2 * old + 1, "x")
-            if okt(2 * old - 1):
-                square_sum(dd[2 * old - 1][:], sq, 2 * old - 1, "q")
+                factor_d(a)
+                factor_d(b)
+                resid(a)
+                whiten(a)
+            if okp(p1):
+                quant_mu(p1)
+                m_um(2 * p1)
+                m_um(2 * p1 + 1)
+                noise(p1)
+                square_sum(ub["m", 2 * p1][:], vm, 2 * p1, "m")
+            if okp(p0):
+                m_mu(p0, 1)
+                m_ux(2 * p0)
+                mu_bias(p0, 2)
+            if okp(p1):
+                square_sum(ub["m", 2 * p1 + 1][:], vm, 2 * p1 + 1, "m")
             if okp(old):
-                t_back(mub, mut, 2 * old, "mu")
-                t_back(isb, ist, 2 * old, "is")
-            if okp(new):
-                m_chan(new, 0)
-                m_ux(2 * new)
-            if okp(old):
-                factor_b(old)
-            if okp(front):
-                exit_hx(2 * front)
-            if n == 2:
-                bias_sum()
-            if okp(old):
-                factor_c(old)
-                noise(2 * old)
-                factor_d(2 * old)
-                factor_d(2 * old + 1)
-            if okp(new):
-                s_mu(new)
-                group_mu(new)
-                square_sum(ub["x", 2 * new][:], vx, 2 * new, "x")
-            if okp(new):
-                m_chan(new, 512)
-            if okp(old):
-                resid(2 * old)
-                sample(2 * old)
-                whiten(2 * old)
-            if okp(new):
-                s_sd(new, 0)
-                s_is(new, 0)
-            if okp(old):
-                t_back(sdb, sdt, 2 * old + 1, "sd")
-                t_back(mub, mut, 2 * old + 1, "mu")
-            if okp(front):
-                t_hx(2 * front + 1)
-            if okp(old):
-                noise(2 * old + 1)
-                square_sum(dd[2 * old][:], sq, 2 * old, "q")
-            if okp(new):
-                quant_mu(new)
-                m_sum(new)
-                m_um(2 * new)
-                m_um(2 * new + 1)
-                s_sd(new, 1)
-            if okp(old):
-                resid(2 * old + 1)
+                sample(a)
+                resid(b)
+                whiten(b)
+                sample(b)
+            if okp(p1):
+                t_mu(2 * p1)
+                t_mu(2 * p1 + 1)
+            if okp(p0):
+                add_lv(2 * p0)
+                square_sum(ub["x", 2 * p0][:], vx, 2 * p0, "x")
             if okp(front):
                 exit_hx(2 * front + 1)
-            if okp(old):
-                sample(2 * old + 1)
-                t_back(isb, ist, 2 * old + 1, "is")
-            if okp(new):
-                t_back(sdb, sdt, 2 * new, "sd")
             if okp(front + 1):
                 t_hx(2 * front + 2)
-            if okp(new):
-                square_sum(ub["m", 2 * new][:], vm, 2 * new, "m")
-                square_sum(ub["m", 2 * new + 1][:], vm, 2 * new + 1, "m")
-                reduce_lv(new)
-            if okp(old):
-                whiten(2 * old + 1)
-            if okp(new):
-                s_is(new, 1)
-                factor_a(new)
-                m_ux(2 * new + 1)
+            if okt(a):
+                square_sum(dd[a][:], sq, a, "q")
+            if okp(p0):
+                m_ux(2 * p0 + 1)
+                square_sum(ub["x", 2 * p0 + 1][:], vx, 2 * p0 + 1, "x")
+            if okp(p0):
+                mu_bias(p0, V_BLOCK)
+            if okp(p0):
+                add_lv(2 * p0 + 1)
+            if okp(front + 1):
+                exit_hx(2 * front + 2)
+                t_hx(2 * front + 3)
 
         lp = const.tile([P, NT], F32, name="lp")
         nc.vector.tensor_tensor(out=lp[:], in0=sl[:], in1=sq[:], op=ALU.add)
         nc.vector.tensor_scalar(
-            out=lp[:], in0=lp[:], scalar1=-0.5, scalar2=base[:, 0:1], op0=ALU.mult, op1=ALU.add
+            out=lp[:], in0=lp[:], scalar1=-0.5, scalar2=-0.5 * N * math.log(2.0 * math.pi), op0=ALU.mult, op1=ALU.add
         )
         nc.sync.dma_start(out=lv, in_=lp[:])

@@ -21,7 +21,7 @@ W = 2 * P
 BETA = 0.99
 FLOOR = 1e-3
 FLOPS = 2 * B * H * (2 * N) + 2 * 2 * B * N * N
-V_BLOCK = 3
+EARLY = (0, 2)
 
 
 def tile_mdn_module_pa_t_kernel(tc, h, W2, b2, x, y, eps, Wv, out_0, out_1):
@@ -130,7 +130,10 @@ def tile_mdn_module_pa_t_kernel(tc, h, W2, b2, x, y, eps, Wv, out_0, out_1):
 
         def t_hx(j):
             q, i = divmod(j, 4)
-            tp[j] = psum.tile([P, 512], F32, name="tp%d" % j, tag="tp")
+            if j == 1:
+                tp[j] = psum.tile([P, 512], F32, name="tp%d" % j, tag="lv", bufs=2)
+            else:
+                tp[j] = psum.tile([P, 512], F32, name="tp%d" % j, tag="tp")
             hw = hq[q][:].bitcast(F32)
             xw = xq[q][:].bitcast(F32)
             for u in range(2):
@@ -196,10 +199,7 @@ def tile_mdn_module_pa_t_kernel(tc, h, W2, b2, x, y, eps, Wv, out_0, out_1):
             if t == 0:
                 mut[p] = work.tile([P, 1024], F32, name="mut%d" % p, tag="mut", bufs=4)
             dst, src = mut[p][:, W * t : W * (t + 1)], mz[p, t // 2][:, W * (t % 2) : W * (t % 2 + 1)]
-            if t == V_BLOCK:
-                nc.vector.tensor_scalar_add(out=dst, in0=src, scalar1=bf32[:, t : t + 1])
-            else:
-                nc.scalar.activation(out=dst, in_=src, func=ACT.Identity, bias=bf32[:, t : t + 1])
+            nc.scalar.activation(out=dst, in_=src, func=ACT.Identity, bias=bf32[:, t : t + 1])
 
         def exps(p):
             sd[p] = work.tile([P, 1024], F32, name="sd%d" % p, tag="sd")
@@ -211,7 +211,7 @@ def tile_mdn_module_pa_t_kernel(tc, h, W2, b2, x, y, eps, Wv, out_0, out_1):
             p, a = divmod(j, 2)
             if a == 0:
                 grp[p] = work.tile([P, 2048], BF16, name="grp%d" % p, tag="grp", align_bytes=64)
-            copy = nc.scalar.copy if j < 2 else nc.vector.tensor_copy
+            copy = nc.scalar.copy if j in EARLY else nc.vector.tensor_copy
             copy(
                 out=grp[p][:].bitcast(F32).rearrange("p (o a r u) -> p o a r u", o=2, a=2, u=2)[:, :, a],
                 in_=tp[j][:].rearrange("p (o u r) -> p o r u", o=2, u=2),
@@ -261,7 +261,7 @@ def tile_mdn_module_pa_t_kernel(tc, h, W2, b2, x, y, eps, Wv, out_0, out_1):
                 nc.sync.dma_start(out=fv[:, 1024 * (c // 2) : 1024 * (c // 2 + 1)], in_=fxp[c // 2][:])
 
         def group_mu(p):
-            gmu[p] = work.tile([P, 1024], BF16, name="gmu%d" % p, tag="gmu", align_bytes=64)
+            gmu[p] = work.tile([P, 1024], BF16, name="gmu%d" % p, tag="gmu", bufs=1, align_bytes=64)
             nc.vector.tensor_copy(
                 out=gmu[p][:].rearrange("p (r t) -> p r t", t=4), in_=mut[p][:].rearrange("p (t r) -> p r t", t=4)
             )
@@ -273,11 +273,14 @@ def tile_mdn_module_pa_t_kernel(tc, h, W2, b2, x, y, eps, Wv, out_0, out_1):
                 out=fxp[p][:], in0=sd[p][:], in1=eq[q][:, 1024 * i : 1024 * (i + 1)], op=ALU.mult
             )
 
-        def whiten(c):
+        def whiten(eng, c, out):
             p, a = divmod(c, 2)
-            nc.gpsimd.tensor_tensor(
-                out=dd[c][:], in0=dd[c][:], in1=isd[p][:, 512 * a : 512 * (a + 1)], op=ALU.mult
-            )
+            eng.tensor_tensor(out=out[:], in0=dd[c][:], in1=isd[p][:, 512 * a : 512 * (a + 1)], op=ALU.mult)
+            dd[c] = out
+
+        def slot(c):
+            dw = work.tile([P, 512], F32, name="dw%d" % c, tag="gmu", bufs=1, align_bytes=64)
+            return dw
 
         def prepare_wv():
             regroup(nc.vector.tensor_copy, wvg[:], wvraw[:].rearrange("p (j c) -> p j c", j=4))
@@ -307,9 +310,9 @@ def tile_mdn_module_pa_t_kernel(tc, h, W2, b2, x, y, eps, Wv, out_0, out_1):
             )
 
         t_hx(0)
-        exit_hx(0)
         t_hx(1)
-        for n in range(NP + 4):
+        exit_hx(0)
+        for n in range(NP + 3):
             front, p0, p1, old = n, n - 1, n - 2, n - 3
             a, b = 2 * old, 2 * old + 1
             if n % 2 == 0:
@@ -330,62 +333,76 @@ def tile_mdn_module_pa_t_kernel(tc, h, W2, b2, x, y, eps, Wv, out_0, out_1):
                 half = w2raw[1][:].rearrange("p (j c) -> p j c", j=4)
                 regroup(nc.vector.tensor_copy, w2g[:, 2048:3072], half[:, :, 0:256])
                 regroup(nc.scalar.copy, w2g[:, 3072:4096], half[:, :, 256:512])
-                prepare_wv()
                 quant_lv()
+                prepare_wv()
             if okp(p1):
                 exps(p1)
-            if okt(a - 1):
-                square_sum(dd[a - 1][:], sq, a - 1, "q")
+            if okt(a - 2):
+                square_sum(dd[a - 2][:], sq, a - 2, "q")
             if okp(p0):
                 m_mu(p0, 0)
-                m_lv(2 * p0)
-                m_lv(2 * p0 + 1)
+                if n > 1:
+                    m_lv(2 * p0)
+                    m_lv(2 * p0 + 1)
                 mu_bias(p0, 0)
                 mu_bias(p0, 1)
+                if n == 1:
+                    m_mu(p0, 1)
+                    m_lv(2 * p0)
+                    m_lv(2 * p0 + 1)
             if okp(old):
                 factor_d(a)
                 factor_d(b)
-                resid(a)
-                whiten(a)
             if okp(p1):
                 quant_mu(p1)
+            if okt(a - 1):
+                whiten(nc.gpsimd, a - 1, slot(a - 1))
+            if okp(p1):
                 m_um(2 * p1)
                 m_um(2 * p1 + 1)
                 noise(p1)
                 square_sum(ub["m", 2 * p1][:], vm, 2 * p1, "m")
             if okp(p0):
-                m_mu(p0, 1)
+                if n > 1:
+                    m_mu(p0, 1)
                 m_ux(2 * p0)
                 mu_bias(p0, 2)
+                mu_bias(p0, 3)
             if okp(p1):
                 square_sum(ub["m", 2 * p1 + 1][:], vm, 2 * p1 + 1, "m")
             if okp(old):
-                sample(a)
-                resid(b)
-                whiten(b)
+                resid(a)
+                whiten(nc.gpsimd, a, dd[a])
+                if b == NT - 1:
+                    resid(b)
+                    sample(a)
+                    whiten(nc.vector, b, dd[b])
+                else:
+                    sample(a)
+                    resid(b)
                 sample(b)
             if okp(p1):
                 t_mu(2 * p1)
                 t_mu(2 * p1 + 1)
-            if okp(p0):
-                add_lv(2 * p0)
-                square_sum(ub["x", 2 * p0][:], vx, 2 * p0, "x")
             if okp(front):
                 exit_hx(2 * front + 1)
             if okp(front + 1):
                 t_hx(2 * front + 2)
-            if okt(a):
-                square_sum(dd[a][:], sq, a, "q")
+            if okp(p0):
+                add_lv(2 * p0)
+                square_sum(ub["x", 2 * p0][:], vx, 2 * p0, "x")
+            if okt(a - 1):
+                square_sum(dd[a - 1][:], sq, a - 1, "q")
             if okp(p0):
                 m_ux(2 * p0 + 1)
                 square_sum(ub["x", 2 * p0 + 1][:], vx, 2 * p0 + 1, "x")
-            if okp(p0):
-                mu_bias(p0, V_BLOCK)
             if okp(p0):
                 add_lv(2 * p0 + 1)
             if okp(front + 1):
                 exit_hx(2 * front + 2)
                 t_hx(2 * front + 3)
+        square_sum(dd[NT - 2][:], sq, NT - 2, "q")
+        square_sum(dd[NT - 1][:], sq, NT - 1, "q")
 
         lp = const.tile([P, NT], F32, name="lp")
         nc.vector.tensor_tensor(out=lp[:], in0=sl[:], in1=sq[:], op=ALU.add)

@@ -178,7 +178,7 @@ def tile_mdn_module_pa_t_kernel(tc, h, W2, b2, x, y, eps, Wv, out_0, out_1):
         def m_ux(j):
             p, a = divmod(j, 2)
             cols = slice(W + P * a, W + P * (a + 1))
-            m_u(("x", j), cod[p][:, cols], scl[p][:, cols], 1 * a)
+            m_u(("x", j), cod[p][:, cols], scl[p][:, cols], 0 * a)
 
         def m_um(j):
             p, a = divmod(j, 2)
@@ -199,7 +199,10 @@ def tile_mdn_module_pa_t_kernel(tc, h, W2, b2, x, y, eps, Wv, out_0, out_1):
             if t == 0:
                 mut[p] = work.tile([P, 1024], F32, name="mut%d" % p, tag="mut", bufs=4)
             dst, src = mut[p][:, W * t : W * (t + 1)], mz[p, t // 2][:, W * (t % 2) : W * (t % 2 + 1)]
-            nc.scalar.activation(out=dst, in_=src, func=ACT.Identity, bias=bf32[:, t : t + 1])
+            if t == 3:
+                nc.vector.tensor_scalar_add(out=dst, in0=src, scalar1=bf32[:, t : t + 1])
+            else:
+                nc.scalar.activation(out=dst, in_=src, func=ACT.Identity, bias=bf32[:, t : t + 1])
 
         def exps(p):
             sd[p] = work.tile([P, 1024], F32, name="sd%d" % p, tag="sd")
@@ -362,27 +365,28 @@ def tile_mdn_module_pa_t_kernel(tc, h, W2, b2, x, y, eps, Wv, out_0, out_1):
                 m_um(2 * p1 + 1)
                 noise(p1)
                 square_sum(ub["m", 2 * p1][:], vm, 2 * p1, "m")
-            if okp(p0):
-                if n > 1:
-                    m_mu(p0, 1)
-                m_ux(2 * p0)
-                mu_bias(p0, 2)
-                mu_bias(p0, 3)
-            if okp(p1):
-                square_sum(ub["m", 2 * p1 + 1][:], vm, 2 * p1 + 1, "m")
             if okp(old):
                 resid(a)
                 whiten(nc.gpsimd, a, dd[a])
                 if b == NT - 1:
                     resid(b)
-                    sample(a)
+                sample(a)
+                if b == NT - 1:
                     whiten(nc.vector, b, dd[b])
-                else:
-                    sample(a)
+            if okp(p1):
+                t_mu(2 * p1)
+            if okp(p0):
+                if n > 1:
+                    m_mu(p0, 1)
+                m_ux(2 * p0)
+                mu_bias(p0, 2)
+            if okp(p1):
+                square_sum(ub["m", 2 * p1 + 1][:], vm, 2 * p1 + 1, "m")
+            if okp(old):
+                if b < NT - 1:
                     resid(b)
                 sample(b)
             if okp(p1):
-                t_mu(2 * p1)
                 t_mu(2 * p1 + 1)
             if okp(front):
                 exit_hx(2 * front + 1)
@@ -397,6 +401,7 @@ def tile_mdn_module_pa_t_kernel(tc, h, W2, b2, x, y, eps, Wv, out_0, out_1):
                 m_ux(2 * p0 + 1)
                 square_sum(ub["x", 2 * p0 + 1][:], vx, 2 * p0 + 1, "x")
             if okp(p0):
+                mu_bias(p0, 3)
                 add_lv(2 * p0 + 1)
             if okp(front + 1):
                 exit_hx(2 * front + 2)

@@ -21,7 +21,7 @@ W = 2 * P
 BETA = 0.99
 FLOOR = 1e-3
 FLOPS = 2 * B * H * (2 * N) + 2 * 2 * B * N * N
-EARLY = (0, 2)
+EARLY = (0, 2, 3)
 
 
 def tile_mdn_module_pa_t_kernel(tc, h, W2, b2, x, y, eps, Wv, out_0, out_1):
@@ -78,6 +78,8 @@ def tile_mdn_module_pa_t_kernel(tc, h, W2, b2, x, y, eps, Wv, out_0, out_1):
         nc.sync.dma_start(out=bl[:], in_=b2[N : 2 * N].partition_broadcast(P))
         load_hx(1, 1)
 
+        zero = const.tile([P, 512], BF16, name="zero")
+        nc.vector.memset(zero[:], 0.0)
         ident = const.tile([P, P], F32, name="ident")
         make_identity(nc, ident[:])
         warm = const.tile([P, 1], F32, name="warm")
@@ -162,7 +164,7 @@ def tile_mdn_module_pa_t_kernel(tc, h, W2, b2, x, y, eps, Wv, out_0, out_1):
         def m_mu(p, b):
             mz[p, b] = psum.tile([P, 512], F32, name="mz%d_%d" % (p, b), tag="mz")
             if b == 0:
-                for d in range(1):
+                for d in range(2):
                     nc.tensor.matmul(mz[p, b][:], lhsT=w2g[:, 0:P], rhs=w2g[:, 0:512], start=True, stop=True)
             for e in range(2):
                 cols = slice(P * (2 * b + e), P * (2 * b + e + 1))
@@ -312,6 +314,9 @@ def tile_mdn_module_pa_t_kernel(tc, h, W2, b2, x, y, eps, Wv, out_0, out_1):
                 op0=ALU.mult, op1=ALU.min,
             )
 
+        heat = psum.tile([P, 512], F32, name="heat", tag="u", bufs=2)
+        for d in range(8):
+            nc.tensor.matmul(heat[:], lhsT=zero[:, 0:P], rhs=zero[:], start=True, stop=True)
         t_hx(0)
         t_hx(1)
         exit_hx(0)

@@ -164,7 +164,7 @@ def tile_mdn_module_pa_t_kernel(tc, h, W2, b2, x, y, eps, Wv, out_0, out_1):
         def m_mu(p, b):
             mz[p, b] = psum.tile([P, 512], F32, name="mz%d_%d" % (p, b), tag="mz")
             if b == 0:
-                for d in range(2):
+                for d in range(2 if p > 0 else 0):
                     nc.tensor.matmul(mz[p, b][:], lhsT=w2g[:, 0:P], rhs=w2g[:, 0:512], start=True, stop=True)
             for e in range(2):
                 cols = slice(P * (2 * b + e), P * (2 * b + e + 1))
@@ -180,7 +180,7 @@ def tile_mdn_module_pa_t_kernel(tc, h, W2, b2, x, y, eps, Wv, out_0, out_1):
         def m_ux(j):
             p, a = divmod(j, 2)
             cols = slice(W + P * a, W + P * (a + 1))
-            m_u(("x", j), cod[p][:, cols], scl[p][:, cols], 0 * a)
+            m_u(("x", j), cod[p][:, cols], scl[p][:, cols], 1 * a)
 
         def m_um(j):
             p, a = divmod(j, 2)
@@ -262,7 +262,9 @@ def tile_mdn_module_pa_t_kernel(tc, h, W2, b2, x, y, eps, Wv, out_0, out_1):
             nc.vector.scalar_tensor_tensor(
                 out=fx_of(c), in0=tm(mub[c]), scalar=sf[:, c : c + 1], in1=fx_of(c), op0=ALU.mult, op1=ALU.add
             )
-            if c % 2 == 1:
+            if c >= NT - 2:
+                nc.sync.dma_start(out=fv[:, 512 * c : 512 * (c + 1)], in_=fxp[c // 2][:, 512 * (c % 2) : 512 * (c % 2 + 1)])
+            elif c % 2 == 1:
                 nc.sync.dma_start(out=fv[:, 1024 * (c // 2) : 1024 * (c // 2 + 1)], in_=fxp[c // 2][:])
 
         def group_mu(p):
@@ -315,7 +317,7 @@ def tile_mdn_module_pa_t_kernel(tc, h, W2, b2, x, y, eps, Wv, out_0, out_1):
             )
 
         heat = psum.tile([P, 512], F32, name="heat", tag="u", bufs=2)
-        for d in range(8):
+        for d in range(5):
             nc.tensor.matmul(heat[:], lhsT=zero[:, 0:P], rhs=zero[:], start=True, stop=True)
         t_hx(0)
         t_hx(1)
@@ -352,6 +354,8 @@ def tile_mdn_module_pa_t_kernel(tc, h, W2, b2, x, y, eps, Wv, out_0, out_1):
                 if n > 1:
                     m_lv(2 * p0)
                     m_lv(2 * p0 + 1)
+                if n == 1:
+                    t_hx(3)
                 mu_bias(p0, 0)
                 mu_bias(p0, 1)
                 if n == 1:
@@ -363,7 +367,7 @@ def tile_mdn_module_pa_t_kernel(tc, h, W2, b2, x, y, eps, Wv, out_0, out_1):
                 factor_d(b)
             if okp(p1):
                 quant_mu(p1)
-            if okt(a - 1):
+            if okt(a - 1) and a - 1 < 30:
                 whiten(nc.gpsimd, a - 1, slot(a - 1))
             if okp(p1):
                 m_um(2 * p1)
@@ -372,12 +376,9 @@ def tile_mdn_module_pa_t_kernel(tc, h, W2, b2, x, y, eps, Wv, out_0, out_1):
                 square_sum(ub["m", 2 * p1][:], vm, 2 * p1, "m")
             if okp(old):
                 resid(a)
-                whiten(nc.gpsimd, a, dd[a])
-                if b == NT - 1:
-                    resid(b)
+                if a < 30:
+                    whiten(nc.gpsimd, a, dd[a])
                 sample(a)
-                if b == NT - 1:
-                    whiten(nc.vector, b, dd[b])
             if okp(p1):
                 t_mu(2 * p1)
             if okp(p0):
@@ -388,9 +389,11 @@ def tile_mdn_module_pa_t_kernel(tc, h, W2, b2, x, y, eps, Wv, out_0, out_1):
             if okp(p1):
                 square_sum(ub["m", 2 * p1 + 1][:], vm, 2 * p1 + 1, "m")
             if okp(old):
-                if b < NT - 1:
-                    resid(b)
+                resid(b)
                 sample(b)
+                for j in (a, b):
+                    if j >= 30:
+                        whiten(nc.vector, j, dd[j])
             if okp(p1):
                 t_mu(2 * p1 + 1)
             if okp(front):
@@ -410,7 +413,8 @@ def tile_mdn_module_pa_t_kernel(tc, h, W2, b2, x, y, eps, Wv, out_0, out_1):
                 add_lv(2 * p0 + 1)
             if okp(front + 1):
                 exit_hx(2 * front + 2)
-                t_hx(2 * front + 3)
+                if n > 0:
+                    t_hx(2 * front + 3)
         square_sum(dd[NT - 2][:], sq, NT - 2, "q")
         square_sum(dd[NT - 1][:], sq, NT - 1, "q")
 

@@ -237,7 +237,7 @@ def tile_mdn_module_pa_t_kernel(tc, h, W2, b2, x, y, eps, Wv, out_0, out_1):
             if a == 0:
                 lv32[p] = work.tile([P, 1024], F32, name="lv%d" % p, tag="lv32")
             nc.vector.scalar_tensor_tensor(
-                out=lv32[p][:, 512 * a : 512 * (a + 1)], in0=lvb[j][:], scalar=1.0, in1=bl[:], op0=ALU.mult, op1=ALU.add,
+                out=lv32[p][:, 512 * a : 512 * (a + 1)], in0=bl[:], scalar=1.0, in1=lvb[j][:], op0=ALU.mult, op1=ALU.add,
                 accum_out=sl[:, j : j + 1],
             )
 
@@ -270,7 +270,8 @@ def tile_mdn_module_pa_t_kernel(tc, h, W2, b2, x, y, eps, Wv, out_0, out_1):
         def group_mu(p):
             gmu[p] = work.tile([P, 1024], BF16, name="gmu%d" % p, tag="gmu", bufs=1, align_bytes=64)
             nc.vector.tensor_copy(
-                out=gmu[p][:].rearrange("p (r t) -> p r t", t=4), in_=mut[p][:].rearrange("p (t r) -> p r t", t=4)
+                out=gmu[p][:].rearrange("p (c k t) -> p c t k", k=4, t=4),
+                in_=mut[p][:].rearrange("p (t c k) -> p c t k", t=4, k=4),
             )
 
         def noise(p):

@@ -348,8 +348,6 @@ def tile_mdn_module_pa_t_kernel(tc, h, W2, b2, x, y, eps, Wv, out_0, out_1):
                 prepare_wv()
             if okp(p1):
                 exps(p1)
-            if okt(a - 2):
-                square_sum(dd[a - 2][:], sq, a - 2, "q")
             if okp(p0):
                 m_mu(p0, 0)
                 if n > 1:
@@ -363,6 +361,8 @@ def tile_mdn_module_pa_t_kernel(tc, h, W2, b2, x, y, eps, Wv, out_0, out_1):
                     m_mu(p0, 1)
                     m_lv(2 * p0)
                     m_lv(2 * p0 + 1)
+            if okt(a - 2):
+                square_sum(dd[a - 2][:], sq, a - 2, "q")
             if okp(old):
                 factor_d(a)
                 factor_d(b)

from contextlib import ExitStack
import math

import concourse.mybir as mybir
from concourse.masks import make_identity

F32 = mybir.dt.float32
BF16 = mybir.dt.bfloat16
U32 = mybir.dt.uint32
U8 = mybir.dt.uint8
FP8X4 = mybir.dt.float8_e4m3fn_x4
ALU = mybir.AluOpType
ACT = mybir.ActivationFunctionType
AX = mybir.AxisListType

P = 128
B, N, H = 4096, 512, 512
NT = B // P
NP = NT // 2
W = 2 * P
BETA = 0.99
FLOOR = 1e-3
FLOPS = 2 * B * H * (2 * N) + 2 * 2 * B * N * N
EARLY = (0, 2, 3)


def tile_mdn_module_pa_t_kernel(tc, h, W2, b2, x, y, eps, Wv, out_0, out_1):
    nc = tc.nc
    hv = h.rearrange("(p j) k -> p (j k)", j=NT)
    xv = x.rearrange("(p j) k -> p (j k)", j=NT)
    yv = y.rearrange("(p j) o k -> p (j o k)", j=NT)
    ev = eps.rearrange("(p j) o k -> p (j o k)", j=NT)
    fv = out_0.rearrange("(p j) o k -> p (j o k)", j=NT)
    lv = out_1.rearrange("(p j) o -> p (j o)", j=NT)

    with ExitStack() as ctx:
        ctx.enter_context(tc.manual_schedule())
        const = ctx.enter_context(tc.tile_pool(name="const", bufs=1))
        stage = ctx.enter_context(tc.tile_pool(name="stage", bufs=1))
        loads = ctx.enter_context(tc.tile_pool(name="loads", bufs=3))
        work = ctx.enter_context(tc.tile_pool(name="work", bufs=3))
        psum = ctx.enter_context(tc.psum_pool(name="psum", bufs=1))

        hq, xq, yq, eq = {}, {}, {}, {}

        def load_hx(q, parts):
            hq[q] = loads.tile([P, 2048], BF16, name="hq%d" % q, tag="hq")
            xq[q] = loads.tile([P, 2048], BF16, name="xq%d" % q, tag="xq")
            w = 2048 // parts
            for s in range(parts):
                lo, hi = w * s, w * (s + 1)
                nc.sync.dma_start(out=hq[q][:, lo:hi], in_=hv[:, 2048 * q + lo : 2048 * q + hi])
                nc.sync.dma_start(out=xq[q][:, lo:hi], in_=xv[:, 2048 * q + lo : 2048 * q + hi])

        def load_ye(q):
            eq[q] = loads.tile([P, 2048], BF16, name="eq%d" % q, tag="eq")
            nc.sync.dma_start(out=eq[q][:], in_=ev[:, 2048 * q : 2048 * (q + 1)])
            yq[q] = loads.tile([P, 2048], BF16, name="yq%d" % q, tag="yq")
            nc.sync.dma_start(out=yq[q][:], in_=yv[:, 2048 * q : 2048 * (q + 1)])

        w2v = W2.rearrange("(u p e) c -> p u e c", u=2, p=P, e=2)
        w2raw = []
        for half in range(2):
            raw = stage.tile([P, 4 * 512], BF16, name="w2raw%d" % half)
            for u in range(2):
                nc.sync.dma_start(
                    out=raw[:, 1024 * u : 1024 * (u + 1)].rearrange("p (e c) -> p e c", e=2),
                    in_=w2v[:, u, :, 512 * half : 512 * (half + 1)],
                )
            w2raw.append(raw)
            if half == 0:
                load_hx(0, 2)
                bm = const.tile([P, 4], BF16, name="bm")
                nc.sync.dma_start(out=bm[:], in_=b2[0:N].rearrange("(p t) -> p t", t=4))
        wvraw = stage.tile([P, 4 * 512], BF16, name="wvraw")
        nc.sync.dma_start(out=wvraw[:], in_=Wv.rearrange("(p t) c -> p (t c)", t=4))
        bl = const.tile([P, N], BF16, name="bl")
        nc.sync.dma_start(out=bl[:], in_=b2[N : 2 * N].partition_broadcast(P))
        load_hx(1, 1)

        zero = const.tile([P, 512], BF16, name="zero")
        nc.vector.memset(zero[:], 0.0)
        ident = const.tile([P, P], F32, name="ident")
        make_identity(nc, ident[:])
        warm = const.tile([P, 1], F32, name="warm")
        nc.vector.memset(warm[:], 0.0)
        nc.scalar.activation(out=warm[:], in_=warm[:], func=ACT.Exp)

        w2c = const.tile([P, 1024], U32, name="w2c", align_bytes=64)
        w2s = const.tile([P, 1024], U8, name="w2s", align_bytes=64)
        wvc = const.tile([P, 512], U32, name="wvc", align_bytes=64)
        wvs = const.tile([P, 512], U8, name="wvs", align_bytes=64)
        w2g = stage.tile([P, 4096], BF16, name="w2g", align_bytes=64)
        wvg = stage.tile([P, 2048], BF16, name="wvg", align_bytes=64)

        def regroup(copy, dst, src):
            copy(
                out=dst.rearrange("p (c k j) -> p c j k", k=4, j=4),
                in_=src.rearrange("p j (c k) -> p c j k", k=4),
            )


        nc.vector.tensor_copy(
            out=w2g[:, 0:2048].rearrange("p (t m j) -> p t m j", t=4, j=4),
            in_=w2raw[0][:].rearrange("p (j m t) -> p t m j", j=4, t=4),
        )
        nc.vector.quantize_mx(out=w2c[:, 0:512].bitcast(FP8X4), scales=w2s[:, 0:512], in_=w2g[:, 0:2048])


        bf32 = const.tile([P, 4], F32, name="bf32")
        nc.vector.tensor_copy(out=bf32[:], in_=bm[:])

        vx = const.tile([P, NT], F32, name="vx")
        vm = const.tile([P, NT], F32, name="vm")
        sq = const.tile([P, NT], F32, name="sq")
        sl = const.tile([P, NT], F32, name="sl")
        sm = const.tile([P, NT], F32, name="sm")
        sr = const.tile([P, NT], F32, name="sr")
        sn = const.tile([P, NT], F32, name="sn")
        sf = const.tile([P, NT], F32, name="sf")

        tp, grp, cod, scl = {}, {}, {}, {}
        mz, ub, lvb, mub = {}, {}, {}, {}
        mut, gmu, cmu, smu = {}, {}, {}, {}
        lv32, sd, isd, dd, fxp = {}, {}, {}, {}, {}

        def okt(j):
            return 0 <= j < NT

        def okp(p):
            return 0 <= p < NP

        def t_hx(j):
            q, i = divmod(j, 4)
            if j == 1:
                tp[j] = psum.tile([P, 512], F32, name="tp%d" % j, tag="lv", bufs=2)
            else:
                tp[j] = psum.tile([P, 512], F32, name="tp%d" % j, tag="tp")
            hw = hq[q][:].bitcast(F32)
            xw = xq[q][:].bitcast(F32)
            for u in range(2):
                nc.tensor.transpose(
                    tp[j][:, u * P : (u + 1) * P], hw[:, 256 * i + P * u : 256 * i + P * (u + 1)], ident[:]
                )
            for u in range(2):
                nc.tensor.transpose(
                    tp[j][:, (2 + u) * P : (3 + u) * P], xw[:, 256 * i + u : 256 * (i + 1) : 2], ident[:]
                )

        def t_mu(c):
            p, a = divmod(c, 2)
            mub[c] = psum.tile([P, 512], F32, name="mub%d" % c, tag="mub", bufs=2)
            for t in range(4):
                nc.tensor.transpose(
                    mub[c][:, P * t : P * (t + 1)], mut[p][:, W * t + P * a : W * t + P * (a + 1)], ident[:]
                )

        def mx(out, lc, ls, rc, rs, start=True, stop=True):
            nc.tensor.matmul_mx(
                out=out, lhsT=lc.bitcast(FP8X4), lhsT_scale=ls, rhs=rc.bitcast(FP8X4), rhs_scale=rs,
                start=start, stop=stop,
            )

        def m_mu(p, b):
            mz[p, b] = psum.tile([P, 512], F32, name="mz%d_%d" % (p, b), tag="mz")
            if b == 0:
                for d in range(2 if p > 0 else 0):
                    nc.tensor.matmul(mz[p, b][:], lhsT=w2g[:, 0:P], rhs=w2g[:, 0:512], start=True, stop=True)
            for e in range(2):
                cols = slice(P * (2 * b + e), P * (2 * b + e + 1))
                mx(mz[p, b][:, W * e : W * (e + 1)], w2c[:, cols], w2s[:, cols], cod[p][:, 0:W], scl[p][:, 0:W])

        def m_u(key, lc, ls, keep=0):
            t0 = psum.tile([P, 512], F32, name="u_%s_%d" % key, tag="u", bufs=2)
            ub[key] = t0
            for d in range(keep):
                nc.tensor.matmul(t0[:], lhsT=w2g[:, 0:P], rhs=w2g[:, 0:512], start=True, stop=True)
            mx(t0[:], lc, ls, wvc[:], wvs[:])

        def m_ux(j):
            p, a = divmod(j, 2)
            cols = slice(W + P * a, W + P * (a + 1))
            m_u(("x", j), cod[p][:, cols], scl[p][:, cols], 1 * a)

        def m_um(j):
            p, a = divmod(j, 2)
            cols = slice(P * a, P * (a + 1))
            m_u(("m", j), cmu[p][:, cols], smu[p][:, cols])

        def m_lv(j):
            p, a = divmod(j, 2)
            rows = slice(P * a, P * (a + 1))
            lvb[j] = psum.tile([P, 512], F32, name="lvb%d" % j, tag="lv", bufs=2)
            mx(lvb[j][:], cod[p][:, rows], scl[p][:, rows], w2c[:, 512:1024], w2s[:, 512:1024])

        def square_sum(src, acc, j, label):
            junk = work.tile([P, 512], BF16, name="junk%s%d" % (label, j), tag="junk", bufs=2)
            nc.scalar.activation(out=junk[:], in_=src, func=ACT.Square, accum_out=acc[:, j : j + 1])

        def mu_bias(p, t):
            if t == 0:
                mut[p] = work.tile([P, 1024], F32, name="mut%d" % p, tag="mut", bufs=4)
            dst, src = mut[p][:, W * t : W * (t + 1)], mz[p, t // 2][:, W * (t % 2) : W * (t % 2 + 1)]
            if t == 3:
                nc.vector.tensor_scalar_add(out=dst, in0=src, scalar1=bf32[:, t : t + 1])
            else:
                nc.scalar.activation(out=dst, in_=src, func=ACT.Identity, bias=bf32[:, t : t + 1])

        def exps(p):
            sd[p] = work.tile([P, 1024], F32, name="sd%d" % p, tag="sd")
            isd[p] = work.tile([P, 1024], F32, name="isd%d" % p, tag="isd")
            nc.scalar.activation(out=sd[p][:], in_=lv32[p][:], func=ACT.Exp, scale=0.5)
            nc.scalar.activation(out=isd[p][:], in_=lv32[p][:], func=ACT.Exp, scale=-0.5)

        def exit_hx(j):
            p, a = divmod(j, 2)
            if a == 0:
                grp[p] = work.tile([P, 2048], BF16, name="grp%d" % p, tag="grp", align_bytes=64)
            copy = nc.scalar.copy if j in EARLY else nc.vector.tensor_copy
            copy(
                out=grp[p][:].bitcast(F32).rearrange("p (o a r u) -> p o a r u", o=2, a=2, u=2)[:, :, a],
                in_=tp[j][:].rearrange("p (o u r) -> p o r u", o=2, u=2),
            )

        def quant_hx(p):
            cod[p] = work.tile([P, 512], U32, name="cod%d" % p, tag="cod", align_bytes=64)
            scl[p] = work.tile([P, 512], U8, name="scl%d" % p, tag="scl", align_bytes=64)
            nc.vector.quantize_mx(out=cod[p][:].bitcast(FP8X4), scales=scl[p][:], in_=grp[p][:])

        def quant_mu(p):
            cmu[p] = work.tile([P, W], U32, name="cmu%d" % p, tag="cmu", align_bytes=64)
            smu[p] = work.tile([P, W], U8, name="smu%d" % p, tag="smu", align_bytes=64)
            nc.vector.quantize_mx(out=cmu[p][:].bitcast(FP8X4), scales=smu[p][:], in_=gmu[p][:])

        def add_lv(j):
            p, a = divmod(j, 2)
            if a == 0:
                lv32[p] = work.tile([P, 1024], F32, name="lv%d" % p, tag="lv32")
            nc.vector.scalar_tensor_tensor(
                out=lv32[p][:, 512 * a : 512 * (a + 1)], in0=bl[:], scalar=1.0, in1=lvb[j][:], op0=ALU.mult, op1=ALU.add,
                accum_out=sl[:, j : j + 1],
            )

        def tm(bank):
            return bank[:].rearrange("p (t m) -> p m t", t=4)

        def mt(ap):
            return ap.rearrange("p (m t) -> p m t", t=4)

        def fx_of(c):
            return mt(fxp[c // 2][:, 512 * (c % 2) : 512 * (c % 2 + 1)])

        def resid(c):
            q, i = divmod(c, 4)
            dd[c] = work.tile([P, 512], F32, name="dd%d" % c, tag="dd", bufs=4)
            nc.vector.scalar_tensor_tensor(
                out=mt(dd[c][:]), in0=tm(mub[c]), scalar=sf[:, c : c + 1], in1=mt(yq[q][:, 512 * i : 512 * (i + 1)]),
                op0=ALU.mult, op1=ALU.subtract,
            )

        def sample(c):
            nc.vector.scalar_tensor_tensor(
                out=fx_of(c), in0=tm(mub[c]), scalar=sf[:, c : c + 1], in1=fx_of(c), op0=ALU.mult, op1=ALU.add
            )
            if c >= NT - 2:
                nc.sync.dma_start(out=fv[:, 512 * c : 512 * (c + 1)], in_=fxp[c // 2][:, 512 * (c % 2) : 512 * (c % 2 + 1)])
            elif c % 2 == 1:
                nc.sync.dma_start(out=fv[:, 1024 * (c // 2) : 1024 * (c // 2 + 1)], in_=fxp[c // 2][:])

        def group_mu(p):
            gmu[p] = work.tile([P, 1024], BF16, name="gmu%d" % p, tag="gmu", bufs=1, align_bytes=64)
            nc.vector.tensor_copy(
                out=gmu[p][:].rearrange("p (c k t) -> p c t k", k=4, t=4),
                in_=mut[p][:].rearrange("p (t c k) -> p c t k", t=4, k=4),
            )

        def noise(p):
            q, i = divmod(p, 2)
            fxp[p] = work.tile([P, 1024], F32, name="fx%d" % p, tag="fx")
            nc.gpsimd.tensor_tensor(
                out=fxp[p][:], in0=sd[p][:], in1=eq[q][:, 1024 * i : 1024 * (i + 1)], op=ALU.mult
            )

        def whiten(eng, c, out):
            p, a = divmod(c, 2)
            eng.tensor_tensor(out=out[:], in0=dd[c][:], in1=isd[p][:, 512 * a : 512 * (a + 1)], op=ALU.mult)
            dd[c] = out

        def slot(c):
            dw = work.tile([P, 512], F32, name="dw%d" % c, tag="gmu", bufs=1, align_bytes=64)
            return dw

        def prepare_wv():
            regroup(nc.vector.tensor_copy, wvg[:], wvraw[:].rearrange("p (j c) -> p j c", j=4))
            nc.vector.quantize_mx(out=wvc[:].bitcast(FP8X4), scales=wvs[:], in_=wvg[:])

        def quant_lv():
            nc.vector.quantize_mx(out=w2c[:, 512:1024].bitcast(FP8X4), scales=w2s[:, 512:1024], in_=w2g[:, 2048:4096])

        def pair_cols(p):
            return slice(2 * p, 2 * p + 2)

        def factor_a(p):
            nc.vector.tensor_scalar_add(out=sm[:, pair_cols(p)], in0=vm[:, pair_cols(p)], scalar1=FLOOR)

        def factor_b(p):
            nc.vector.reciprocal(out=sr[:, pair_cols(p)], in_=sm[:, pair_cols(p)])

        def factor_c(p):
            nc.vector.tensor_scalar(
                out=sn[:, pair_cols(p)], in0=vx[:, pair_cols(p)], scalar1=FLOOR, scalar2=BETA, op0=ALU.add, op1=ALU.mult
            )

        def factor_d(j):
            nc.vector.tensor_scalar(
                out=sf[:, j : j + 1], in0=sn[:, j : j + 1], scalar1=sr[:, j : j + 1], scalar2=1.0,
                op0=ALU.mult, op1=ALU.min,
            )

        heat = psum.tile([P, 512], F32, name="heat", tag="u", bufs=2)
        for d in range(5):
            nc.tensor.matmul(heat[:], lhsT=zero[:, 0:P], rhs=zero[:], start=True, stop=True)
        t_hx(0)
        t_hx(1)
        exit_hx(0)
        for n in range(NP + 3):
            front, p0, p1, old = n, n - 1, n - 2, n - 3
            a, b = 2 * old, 2 * old + 1
            if n % 2 == 0:
                if n // 2 < NT // 4:
                    load_ye(n // 2)
                if n // 2 + 2 < NT // 4:
                    load_hx(n // 2 + 2, 1)
            if okp(old):
                factor_a(old)
                factor_c(old)
            if okp(p1):
                group_mu(p1)
            if okp(old):
                factor_b(old)
            if okp(p0):
                quant_hx(p0)
            if n == 1:
                half = w2raw[1][:].rearrange("p (j c) -> p j c", j=4)
                regroup(nc.vector.tensor_copy, w2g[:, 2048:3072], half[:, :, 0:256])
                regroup(nc.scalar.copy, w2g[:, 3072:4096], half[:, :, 256:512])
                quant_lv()
                prepare_wv()
            if okp(p1):
                exps(p1)
            if okp(p0):
                m_mu(p0, 0)
                if n > 1:
                    m_lv(2 * p0)
                    m_lv(2 * p0 + 1)
                if n == 1:
                    t_hx(3)
                mu_bias(p0, 0)
                mu_bias(p0, 1)
                if n == 1:
                    m_mu(p0, 1)
                    m_lv(2 * p0)
                    m_lv(2 * p0 + 1)
            if okt(a - 2):
                square_sum(dd[a - 2][:], sq, a - 2, "q")
            if okp(old):
                factor_d(a)
                factor_d(b)
            if okp(p1):
                quant_mu(p1)
            if okt(a - 1) and a - 1 < 30:
                whiten(nc.gpsimd, a - 1, slot(a - 1))
            if okp(p1):
                m_um(2 * p1)
                m_um(2 * p1 + 1)
                noise(p1)
                square_sum(ub["m", 2 * p1][:], vm, 2 * p1, "m")
            if okp(old):
                resid(a)
                if a < 30:
                    whiten(nc.gpsimd, a, dd[a])
                sample(a)
            if okp(p1):
                t_mu(2 * p1)
            if okp(p0):
                if n > 1:
                    m_mu(p0, 1)
                m_ux(2 * p0)
                mu_bias(p0, 2)
            if okp(p1):
                square_sum(ub["m", 2 * p1 + 1][:], vm, 2 * p1 + 1, "m")
            if okp(old):
                resid(b)
                sample(b)
                for j in (a, b):
                    if j >= 30:
                        whiten(nc.vector, j, dd[j])
            if okp(p1):
                t_mu(2 * p1 + 1)
            if okp(front):
                exit_hx(2 * front + 1)
            if okp(front + 1):
                t_hx(2 * front + 2)
            if okp(p0):
                add_lv(2 * p0)
                square_sum(ub["x", 2 * p0][:], vx, 2 * p0, "x")
            if okt(a - 1):
                square_sum(dd[a - 1][:], sq, a - 1, "q")
            if okp(p0):
                m_ux(2 * p0 + 1)
                square_sum(ub["x", 2 * p0 + 1][:], vx, 2 * p0 + 1, "x")
            if okp(p0):
                mu_bias(p0, 3)
                add_lv(2 * p0 + 1)
            if okp(front + 1):
                exit_hx(2 * front + 2)
                if n > 0:
                    t_hx(2 * front + 3)
        square_sum(dd[NT - 2][:], sq, NT - 2, "q")
        square_sum(dd[NT - 1][:], sq, NT - 1, "q")

        lp = const.tile([P, NT], F32, name="lp")
        nc.vector.tensor_tensor(out=lp[:], in0=sl[:], in1=sq[:], op=ALU.add)
        nc.vector.tensor_scalar(
            out=lp[:], in0=lp[:], scalar1=-0.5, scalar2=-0.5 * N * math.log(2.0 * math.pi), op0=ALU.mult, op1=ALU.add
        )
        nc.sync.dma_start(out=lv, in_=lp[:])
